import numpy as np
import ml_dtypes


def mxq(x, axis, fmt="e4m3"):
    dtype, down = {"e4m3": (ml_dtypes.float8_e4m3fn, 7), "e5m2": (ml_dtypes.float8_e5m2, 14)}[fmt]
    v = np.moveaxis(np.asarray(x, np.float32).astype(ml_dtypes.bfloat16).astype(np.float64), axis, -1)
    blocks = v.reshape(v.shape[:-1] + (-1, 32))
    amax = np.abs(blocks).max(-1, keepdims=True)
    byte = np.maximum(np.where(amax > 0, np.frexp(amax)[1] - 1 + 127, 0) - down, 1)
    scale = np.exp2(byte - 127.0)
    codes = (blocks / scale).astype(np.float32).astype(dtype).astype(np.float64)
    return np.moveaxis((codes * scale).reshape(v.shape), -1, axis)


WIDE = False


def mx_kscale(k):
    if not WIDE:
        return np.ones(k)
    levels = np.array([10, -10, 5, -5, 0])
    a = np.random.permutation(np.resize(levels, k // 512 * 4)).reshape(k // 512, 4)
    idx = np.arange(k)
    return np.exp2(a[idx // 512, idx % 128 // 32])


BF16 = ml_dtypes.bfloat16


def bf(x):
    return np.asarray(x, np.float32).astype(BF16)


def f64(x):
    return np.asarray(x).astype(np.float64)


E2M1 = np.array([0.0, 0.5, 1.0, 1.5, 2.0, 3.0, 4.0, 6.0, -0.0, -0.5, -1.0, -1.5, -2.0, -3.0, -4.0, -6.0])


def pack_weight(w, fmt):
    k, n = w.shape
    w = f64(bf(w)).reshape(k // 32, 32, n)
    amax = np.abs(w).max(1)
    if fmt == "e4m3":
        byte = np.frexp(amax)[1] - 1 + 127 - 7
    else:
        mant, ex = np.frexp(amax / 6.0)
        byte = np.where(mant > 0.5, ex, ex - 1) + 127
    byte = np.clip(np.where(amax > 0, byte, 1), 1, 254)
    scaled = (w * np.exp2(127.0 - byte)[:, None, :]).reshape(k, n).astype(np.float32)
    by_word = np.ascontiguousarray(scaled.reshape(k // 512, 128, 4, n).transpose(0, 1, 3, 2))
    if fmt == "e4m3":
        words = by_word.astype(ml_dtypes.float8_e4m3fn).view(np.uint8)
    else:
        c = by_word.astype(ml_dtypes.float4_e2m1fn).view(np.uint8) & 0xF
        words = c[..., 0::2] | (c[..., 1::2] << 4)
    return np.ascontiguousarray(words), np.ascontiguousarray(byte.astype(np.uint8).reshape(k // 512, 16, n))


def unpack_weight(words, scales, fmt):
    g, p, n, _ = words.shape
    if fmt == "e4m3":
        vals = np.ascontiguousarray(words).view(ml_dtypes.float8_e4m3fn).astype(np.float64)
    else:
        nib = np.empty((g, p, n, 4), np.uint8)
        nib[..., 0::2] = words & 0xF
        nib[..., 1::2] = words >> 4
        vals = E2M1[nib]
    vals = vals * np.repeat(np.exp2(scales.astype(np.float64) - 127.0), 8, axis=1)[..., None]
    return vals.transpose(0, 1, 3, 2).reshape(g * 512, n)


N, S, F, M0, M1, M2 = 1024, 288, 512, 128, 64, 32
MULS_LS = ((M0, 0), (M1, 1), (M2, 2))
NI = sum(m for m, l in MULS_LS)
ED = sum(m * (2 * l + 1) for m, l in MULS_LS)
C = S + NI
EPS = 1e-5
FMT = "e4m3"


def silu(v):
    return v / (1.0 + np.exp(-v))


def _blocks(x):
    outs, off = [], 0
    for mul, l in MULS_LS:
        d = 2 * l + 1
        outs.append(x[:, off:off + mul * d].reshape(x.shape[0], mul, d))
        off += mul * d
    return outs


def setup_inputs():
    s = np.array(mx_kscale(C), dtype=np.float64)
    s[S:] = 1.0
    xs = np.random.standard_normal((N, S)) + 0.5 * np.random.standard_normal((N, 1))
    xe = np.random.standard_normal((N, ED))
    xe[:, :M0] += 0.5 * np.random.standard_normal((N, 1))
    ln_w = bf((1.0 + 0.1 * np.random.standard_normal(S)) * s[:S])
    ln_b = bf(0.2 * np.random.standard_normal(S) * s[:S])
    W1_words, W1_scales = pack_weight(np.random.standard_normal((C, F)) / np.sqrt(C) / s[:, None], FMT)
    b1 = bf(0.2 * np.random.standard_normal(F))
    W2_words, W2_scales = pack_weight(np.random.standard_normal((F, C)) * 1.5 / np.sqrt(F), FMT)
    b2 = bf(0.2 * np.random.standard_normal(C))
    return {"node_scalar": bf(xs),
            "node_equi": bf(xe),
            "ln_w": ln_w,
            "ln_b": ln_b,
            "W1_words": W1_words,
            "W1_scales": W1_scales,
            "b1": b1,
            "W2_words": W2_words,
            "W2_scales": W2_scales,
            "b2": b2}


def reference(node_scalar, node_equi, ln_w, ln_b, W1_words, W1_scales, b1, W2_words, W2_scales, b2):
    node_scalar, node_equi = f64(node_scalar), f64(node_equi)
    mu = node_scalar.mean(-1, keepdims=True)
    var = node_scalar.var(-1, keepdims=True)
    ns = (node_scalar - mu) / np.sqrt(var + EPS) * f64(ln_w) + f64(ln_b)
    eb = []
    for (mul, l), blk in zip(MULS_LS, _blocks(node_equi)):
        if l == 0:
            blk = blk - blk.mean(axis=1, keepdims=True)
        norm2 = (blk * blk).sum(-1, keepdims=True).mean(axis=1, keepdims=True)
        eb.append(blk / np.sqrt(norm2 + EPS))
    inv = np.concatenate([(blk * blk).sum(-1) / np.sqrt(2 * l + 1) for (mul, l), blk in zip(MULS_LS, eb)], axis=-1)
    cat = np.concatenate([ns, inv], axis=-1)
    a = (mxq(cat, 1, "e4m3") @ unpack_weight(W1_words, W1_scales, FMT)) + f64(b1)
    h = (mxq(silu(a), 1, "e4m3") @ unpack_weight(W2_words, W2_scales, FMT)) + f64(b2)
    d_scalar, gate = h[:, :S], h[:, S:]
    gparts = np.split(gate, [M0, M0 + M1], axis=-1)
    n = node_scalar.shape[0]
    d_equi = np.concatenate([(blk * g[:, :, None]).reshape(n, -1) for blk, g in zip(eb, gparts)], axis=-1)
    return np.concatenate([node_scalar + d_scalar, node_equi + d_equi], axis=-1)

@@ -1,0 +1,263 @@
+import math
+from contextlib import ExitStack
+
+import concourse.mybir as mybir
+from concourse.masks import make_identity
+
+F32 = mybir.dt.float32
+BF16 = mybir.dt.bfloat16
+I32 = mybir.dt.int32
+U32 = mybir.dt.uint32
+U8 = mybir.dt.uint8
+FP8X4 = mybir.dt.float8_e4m3fn_x4
+ALU = mybir.AluOpType
+ACT = mybir.ActivationFunctionType
+AXIS = mybir.AxisListType
+
+P = 128
+ROWS = 1024
+TILES = ROWS // P
+PAIRS = TILES // 2
+S = 288
+M0, M1, M2 = 128, 64, 32
+D1, D2 = 3, 5
+E1 = M0
+E2 = M0 + M1 * D1
+ED = E2 + M2 * D2
+NI = M0 + M1 + M2
+C = S + NI
+EPS = 1e-5
+
+FLOPS = 2 * 2 * ROWS * C * C
+
+
+def weight_tiles(nc, keep, name):
+    words = keep.tile([P, 4 * C], U8, name=name + "_words", align_bytes=64)
+    plane = keep.tile([P, C], U8, name=name + "_plane", align_bytes=64)
+    nc.vector.memset(plane[:].bitcast(I32), 0)
+    return words, plane
+
+
+def transpose_and_quantise(nc, work, psum_t, ident, src, pair, codes, plane):
+    turned = psum_t.tile([P, 2, 2 * P], F32, name="turned")
+    for half in range(2):
+        words = src[:, 2 * pair + half, :].bitcast(F32)
+        for u in range(2):
+            nc.tensor.transpose(turned[:, u, half * P : (half + 1) * P], words[:, u : C // 2 : 2], ident[:])
+    grouped = work.tile([P, 2 * P, 4], BF16, name="grouped", align_bytes=64)
+    nc.scalar.copy(
+        out=grouped[:].rearrange("p r t -> p (r t)").bitcast(F32).rearrange("p (r u) -> p r u", u=2),
+        in_=turned[:].rearrange("p u r -> p r u"),
+    )
+    nc.vector.quantize_mx(
+        out=codes.bitcast(FP8X4),
+        scales=plane,
+        in_=grouped[:].rearrange("p r t -> p (r t)"),
+    )
+
+
+def tile_interactionblock_kernel(
+    tc, node_scalar, node_equi, ln_w, ln_b, W1_words, W1_scales, b1, W2_words, W2_scales, b2, out
+):
+    nc = tc.nc
+    xs_dram = node_scalar.rearrange("(p i) s -> p i s", i=TILES)
+    xe_dram = node_equi.rearrange("(p i) e -> p i e", i=TILES)
+    out_dram = out.rearrange("(p i) c -> p i c", i=TILES)
+
+    with ExitStack() as ctx:
+        keep = ctx.enter_context(tc.tile_pool(name="keep", bufs=1))
+        work = ctx.enter_context(tc.tile_pool(name="work", bufs=3))
+        psum_t = ctx.enter_context(tc.psum_pool(name="psum_t", bufs=2))
+        psum_mm = ctx.enter_context(tc.psum_pool(name="psum_mm", bufs=6))
+
+        eps_col = keep.tile([P, 1], F32, name="eps_col")
+        nc.vector.memset(eps_col[:], EPS)
+        one_col = keep.tile([P, 1], F32, name="one_col")
+        nc.vector.memset(one_col[:], 1.0)
+        warm = keep.tile([P, 1], F32, name="warm")
+        nc.scalar.activation(out=warm[:], in_=one_col[:], func=ACT.Sqrt)
+        ones_sq = keep.tile([P, P], BF16, name="ones_sq")
+        nc.vector.memset(ones_sq[:], 1.0)
+        vec_rows = keep.tile([P, 4, C], BF16, name="vec_rows")
+        nc.vector.memset(vec_rows[:].rearrange("p v c -> p (v c)").bitcast(I32), 0)
+        w1_words, w1_plane = weight_tiles(nc, keep, "w1")
+        w2_words, w2_plane = weight_tiles(nc, keep, "w2")
+        ident = keep.tile([P, P], F32, name="ident")
+        make_identity(nc, ident[:])
+
+        x_s = keep.tile([P, TILES, S], BF16, name="x_s")
+        x_e = keep.tile([P, TILES, ED], BF16, name="x_e")
+        half_tiles = TILES // 2
+        for lo in (0, half_tiles):
+            nc.sync.dma_start(out=x_s[:, lo : lo + half_tiles, :], in_=xs_dram[:, lo : lo + half_tiles, :])
+            nc.sync.dma_start(out=x_e[:, lo : lo + half_tiles, :], in_=xe_dram[:, lo : lo + half_tiles, :])
+        for v, vec in enumerate((ln_w, ln_b, b1, b2)):
+            width = vec.shape[0]
+            nc.scalar.dma_start(out=vec_rows[0:1, v, 0:width], in_=vec.rearrange("(o c) -> o c", o=1))
+        for words, plane, words_dram, scales_dram in (
+            (w1_words, w1_plane, W1_words, W1_scales),
+            (w2_words, w2_plane, W2_words, W2_scales),
+        ):
+            nc.sync.dma_start(out=words[:].bitcast(I32), in_=words_dram[0].rearrange("p n t -> p (n t)").bitcast(I32))
+            for q in range(4):
+                nc.sync.dma_start(
+                    out=plane[32 * q : 32 * q + 4, :].bitcast(I32),
+                    in_=scales_dram[0, 4 * q : 4 * q + 4, :].bitcast(I32),
+                )
+
+        vec_bc = keep.tile([P, 4, C], F32, name="vec_bc")
+        for v, vec in enumerate((ln_w, ln_b, b1, b2)):
+            width = vec.shape[0]
+            spread = psum_mm.tile([P, C], F32, name="spread", tag="acc")
+            nc.tensor.matmul(out=spread[:], lhsT=ones_sq[:], rhs=vec_rows[:, v, :], start=True, stop=True)
+            nc.scalar.copy(out=vec_bc[:, v, 0:width], in_=spread[:, 0:width])
+        lnw_bc = vec_bc[:, 0, 0:S]
+        lnb_bc = vec_bc[:, 1, 0:S]
+        b1_bc = vec_bc[:, 2, :]
+        b2_bc = vec_bc[:, 3, :]
+
+        bn = keep.tile([P, 2, TILES, 6], F32, name="bn")
+        mean_var = keep.tile([P, 2, TILES, 2], F32, name="mean_var")
+        for i in range(TILES):
+            nc.vector.bn_stats(out=bn[:, 0, i, :], in_=x_s[:, i, :])
+            nc.vector.bn_stats(out=bn[:, 1, i, :], in_=x_e[:, i, 0:M0])
+        for i in range(TILES):
+            nc.vector.bn_aggr(out=mean_var[:, 0, i, :], in_=bn[:, 0, i, :])
+            nc.vector.bn_aggr(out=mean_var[:, 1, i, :], in_=bn[:, 1, i, :])
+        squares = keep.tile([P, TILES, ED - E1], F32, name="squares")
+        square_sum = keep.tile([P, 2, TILES], F32, name="square_sum")
+        for i in range(TILES):
+            nc.scalar.activation(
+                out=squares[:, i, 0 : E2 - E1], in_=x_e[:, i, E1:E2], func=ACT.Square,
+                scale=D1**-0.25, accum_out=square_sum[:, 0, i : i + 1],
+            )
+            nc.scalar.activation(
+                out=squares[:, i, E2 - E1 :], in_=x_e[:, i, E2:ED], func=ACT.Square,
+                scale=D2**-0.25, accum_out=square_sum[:, 1, i : i + 1],
+            )
+        std = keep.tile([P, 4, TILES], F32, name="std")
+        nc.scalar.activation(out=std[:, 0:2, :], in_=mean_var[:, :, :, 1], func=ACT.Sqrt, bias=eps_col[:])
+        nc.scalar.activation(
+            out=std[:, 2, :], in_=square_sum[:, 0, :], func=ACT.Sqrt, scale=math.sqrt(D1) / M1, bias=eps_col[:]
+        )
+        nc.scalar.activation(
+            out=std[:, 3, :], in_=square_sum[:, 1, :], func=ACT.Sqrt, scale=math.sqrt(D2) / M2, bias=eps_col[:]
+        )
+        rstd = keep.tile([P, 4, TILES], F32, name="rstd")
+        nc.vector.reciprocal(out=rstd[:], in_=std[:])
+        shift0 = keep.tile([P, TILES], F32, name="shift0")
+        nc.vector.scalar_tensor_tensor(
+            out=shift0[:], in0=mean_var[:, 1, :, 0], scalar=-1.0, in1=rstd[:, 1, :], op0=ALU.mult, op1=ALU.mult
+        )
+        rvar = keep.tile([P, 2, TILES], F32, name="rvar")
+        nc.vector.tensor_tensor(out=rvar[:], in0=rstd[:, 2:4, :], in1=rstd[:, 2:4, :], op=ALU.mult)
+
+        xs_b2 = keep.tile([P, TILES, S], F32, name="xs_b2")
+        nc.gpsimd.tensor_tensor(
+            out=xs_b2[:], in0=x_s[:], in1=b2_bc[:, 0:S].unsqueeze(1).to_broadcast([P, TILES, S]), op=ALU.add
+        )
+
+        cat = keep.tile([P, TILES, C], BF16, name="cat", align_bytes=64)
+        for i in range(TILES):
+            centred = work.tile([P, S], F32, name="centred")
+            nc.vector.scalar_tensor_tensor(
+                out=centred[:], in0=x_s[:, i, :], scalar=mean_var[:, 0, i, 0:1], in1=lnw_bc,
+                op0=ALU.subtract, op1=ALU.mult,
+            )
+            nc.vector.scalar_tensor_tensor(
+                out=cat[:, i, 0:S], in0=centred[:], scalar=rstd[:, 0, i : i + 1], in1=lnb_bc,
+                op0=ALU.mult, op1=ALU.add,
+            )
+            nc.scalar.activation(
+                out=cat[:, i, S : S + M0], in_=x_e[:, i, 0:M0], func=ACT.Square,
+                scale=rstd[:, 1, i : i + 1], bias=shift0[:, i : i + 1],
+            )
+        norms = keep.tile([P, TILES, M1 + M2], F32, name="norms")
+        nc.vector.tensor_reduce(
+            out=norms[:, :, 0:M1], in_=squares[:, :, 0 : E2 - E1].rearrange("p i (c d) -> p i c d", d=D1),
+            axis=AXIS.X, op=ALU.add,
+        )
+        nc.vector.tensor_reduce(
+            out=norms[:, :, M1:], in_=squares[:, :, E2 - E1 :].rearrange("p i (c d) -> p i c d", d=D2),
+            axis=AXIS.X, op=ALU.add,
+        )
+        nc.vector.tensor_tensor(
+            out=cat[:, :, S + M0 : S + M0 + M1], in0=norms[:, :, 0:M1],
+            in1=rvar[:, 0, :].unsqueeze(2).to_broadcast([P, TILES, M1]), op=ALU.mult,
+        )
+        nc.vector.tensor_tensor(
+            out=cat[:, :, S + M0 + M1 :], in0=norms[:, :, M1:],
+            in1=rvar[:, 1, :].unsqueeze(2).to_broadcast([P, TILES, M2]), op=ALU.mult,
+        )
+
+        blocks = ((0, M0, 1), (M0, M0 + M1, 2), (M0 + M1, NI, 3))
+        gate_bias = keep.tile([P, TILES, NI], F32, name="gate_bias")
+        for i in range(TILES):
+            for lo, hi, kind in blocks:
+                nc.scalar.activation(
+                    out=gate_bias[:, i, lo:hi], in_=b2_bc[:, S + lo : S + hi], func=ACT.Identity,
+                    scale=rstd[:, kind, i : i + 1], bias=one_col[:],
+                )
+
+        codes = keep.tile([P, 2, PAIRS, 2 * P], U32, name="codes", align_bytes=64)
+        planes = keep.tile([P, 2, PAIRS, 2 * P], U8, name="planes", align_bytes=64)
+        hidden = keep.tile([P, TILES, C], BF16, name="hidden", align_bytes=64)
+        for pair in range(PAIRS):
+            transpose_and_quantise(nc, work, psum_t, ident, cat, pair, codes[:, 0, pair, :], planes[:, 0, pair, :])
+            for half in range(2):
+                i = 2 * pair + half
+                acc = psum_mm.tile([P, C], F32, name="acc")
+                nc.tensor.matmul_mx(
+                    out=acc[:],
+                    lhsT=codes[:, 0, pair, half * P : (half + 1) * P].bitcast(FP8X4),
+                    lhsT_scale=planes[:, 0, pair, half * P : (half + 1) * P],
+                    rhs=w1_words[:].bitcast(FP8X4),
+                    rhs_scale=w1_plane[:],
+                    start=True,
+                    stop=True,
+                )
+                biased = work.tile([P, C], F32, name="biased")
+                nc.vector.tensor_tensor(out=biased[:], in0=acc[:], in1=b1_bc, op=ALU.add)
+                nc.scalar.activation(out=hidden[:, i, :], in_=biased[:], func=ACT.Silu)
+
+        res = keep.tile([P, TILES, S + ED], F32, name="res")
+        for pair in range(PAIRS):
+            transpose_and_quantise(nc, work, psum_t, ident, hidden, pair, codes[:, 1, pair, :], planes[:, 1, pair, :])
+            for half in range(2):
+                i = 2 * pair + half
+                acc = psum_mm.tile([P, C], F32, name="acc")
+                nc.tensor.matmul_mx(
+                    out=acc[:],
+                    lhsT=codes[:, 1, pair, half * P : (half + 1) * P].bitcast(FP8X4),
+                    lhsT_scale=planes[:, 1, pair, half * P : (half + 1) * P],
+                    rhs=w2_words[:].bitcast(FP8X4),
+                    rhs_scale=w2_plane[:],
+                    start=True,
+                    stop=True,
+                )
+                nc.vector.tensor_tensor(out=res[:, i, 0:S], in0=acc[:, 0:S], in1=xs_b2[:, i, :], op=ALU.add)
+                factor = work.tile([P, NI], F32, name="factor")
+                for lo, hi, kind in blocks:
+                    nc.vector.scalar_tensor_tensor(
+                        out=factor[:, lo:hi], in0=acc[:, S + lo : S + hi], scalar=rstd[:, kind, i : i + 1],
+                        in1=gate_bias[:, i, lo:hi], op0=ALU.mult, op1=ALU.add,
+                    )
+                mean0 = mean_var[:, 1, i, 0:1]
+                nc.vector.scalar_tensor_tensor(
+                    out=res[:, i, S : S + M0], in0=x_e[:, i, 0:M0], scalar=mean0, in1=factor[:, 0:M0],
+                    op0=ALU.subtract, op1=ALU.mult,
+                )
+                nc.vector.tensor_tensor(
+                    out=res[:, i, S + E1 : S + E2].rearrange("p (c d) -> p c d", d=D1),
+                    in0=x_e[:, i, E1:E2].rearrange("p (c d) -> p c d", d=D1),
+                    in1=factor[:, M0 : M0 + M1].unsqueeze(2).to_broadcast([P, M1, D1]),
+                    op=ALU.mult,
+                )
+                nc.vector.tensor_tensor(
+                    out=res[:, i, S + E2 :].rearrange("p (c d) -> p c d", d=D2),
+                    in0=x_e[:, i, E2:ED].rearrange("p (c d) -> p c d", d=D2),
+                    in1=factor[:, M0 + M1 :].unsqueeze(2).to_broadcast([P, M2, D2]),
+                    op=ALU.mult,
+                )
+                nc.vector.tensor_scalar_add(out=res[:, i, S : S + M0], in0=res[:, i, S : S + M0], scalar1=mean0)
+                nc.sync.dma_start(out=out_dram[:, i, :], in_=res[:, i, :])

@@ -31,31 +31,6 @@ EPS = 1e-5
 FLOPS = 2 * 2 * ROWS * C * C
 
 
-def weight_tiles(nc, keep, name):
-    words = keep.tile([P, 4 * C], U8, name=name + "_words", align_bytes=64)
-    plane = keep.tile([P, C], U8, name=name + "_plane", align_bytes=64)
-    nc.vector.memset(plane[:].bitcast(I32), 0)
-    return words, plane
-
-
-def transpose_and_quantise(nc, work, psum_t, ident, src, pair, codes, plane):
-    turned = psum_t.tile([P, 2, 2 * P], F32, name="turned")
-    for half in range(2):
-        words = src[:, 2 * pair + half, :].bitcast(F32)
-        for u in range(2):
-            nc.tensor.transpose(turned[:, u, half * P : (half + 1) * P], words[:, u : C // 2 : 2], ident[:])
-    grouped = work.tile([P, 2 * P, 4], BF16, name="grouped", align_bytes=64)
-    nc.scalar.copy(
-        out=grouped[:].rearrange("p r t -> p (r t)").bitcast(F32).rearrange("p (r u) -> p r u", u=2),
-        in_=turned[:].rearrange("p u r -> p r u"),
-    )
-    nc.vector.quantize_mx(
-        out=codes.bitcast(FP8X4),
-        scales=plane,
-        in_=grouped[:].rearrange("p r t -> p (r t)"),
-    )
-
-
 def tile_interactionblock_kernel(
     tc, node_scalar, node_equi, ln_w, ln_b, W1_words, W1_scales, b1, W2_words, W2_scales, b2, out
 ):
@@ -67,66 +42,61 @@ def tile_interactionblock_kernel(
     with ExitStack() as ctx:
         keep = ctx.enter_context(tc.tile_pool(name="keep", bufs=1))
         work = ctx.enter_context(tc.tile_pool(name="work", bufs=3))
+        psum_ln = ctx.enter_context(tc.psum_pool(name="psum_ln", bufs=1))
         psum_t = ctx.enter_context(tc.psum_pool(name="psum_t", bufs=2))
-        psum_mm = ctx.enter_context(tc.psum_pool(name="psum_mm", bufs=6))
-
-        eps_col = keep.tile([P, 1], F32, name="eps_col")
-        nc.vector.memset(eps_col[:], EPS)
-        one_col = keep.tile([P, 1], F32, name="one_col")
-        nc.vector.memset(one_col[:], 1.0)
-        warm = keep.tile([P, 1], F32, name="warm")
-        nc.scalar.activation(out=warm[:], in_=one_col[:], func=ACT.Sqrt)
-        ones_sq = keep.tile([P, P], BF16, name="ones_sq")
-        nc.vector.memset(ones_sq[:], 1.0)
-        vec_rows = keep.tile([P, 4, C], BF16, name="vec_rows")
-        nc.vector.memset(vec_rows[:].rearrange("p v c -> p (v c)").bitcast(I32), 0)
-        w1_words, w1_plane = weight_tiles(nc, keep, "w1")
-        w2_words, w2_plane = weight_tiles(nc, keep, "w2")
-        ident = keep.tile([P, P], F32, name="ident")
-        make_identity(nc, ident[:])
+        psum_mm = ctx.enter_context(tc.psum_pool(name="psum_mm", bufs=4))
+        ctx.enter_context(tc.manual_schedule())
 
         x_s = keep.tile([P, TILES, S], BF16, name="x_s")
         x_e = keep.tile([P, TILES, ED], BF16, name="x_e")
-        half_tiles = TILES // 2
-        for lo in (0, half_tiles):
-            nc.sync.dma_start(out=x_s[:, lo : lo + half_tiles, :], in_=xs_dram[:, lo : lo + half_tiles, :])
-            nc.sync.dma_start(out=x_e[:, lo : lo + half_tiles, :], in_=xe_dram[:, lo : lo + half_tiles, :])
-        for v, vec in enumerate((ln_w, ln_b, b1, b2)):
-            width = vec.shape[0]
-            nc.scalar.dma_start(out=vec_rows[0:1, v, 0:width], in_=vec.rearrange("(o c) -> o c", o=1))
-        for words, plane, words_dram, scales_dram in (
-            (w1_words, w1_plane, W1_words, W1_scales),
-            (w2_words, w2_plane, W2_words, W2_scales),
-        ):
-            nc.sync.dma_start(out=words[:].bitcast(I32), in_=words_dram[0].rearrange("p n t -> p (n t)").bitcast(I32))
-            for q in range(4):
-                nc.sync.dma_start(
-                    out=plane[32 * q : 32 * q + 4, :].bitcast(I32),
-                    in_=scales_dram[0, 4 * q : 4 * q + 4, :].bitcast(I32),
-                )
+        for pair in range(PAIRS):
+            two = slice(2 * pair, 2 * pair + 2)
+            nc.sync.dma_start(out=x_s[:, two, :], in_=xs_dram[:, two, :])
+            nc.sync.dma_start(out=x_e[:, two, :], in_=xe_dram[:, two, :])
 
-        vec_bc = keep.tile([P, 4, C], F32, name="vec_bc")
-        for v, vec in enumerate((ln_w, ln_b, b1, b2)):
-            width = vec.shape[0]
-            spread = psum_mm.tile([P, C], F32, name="spread", tag="acc")
+        vec_rows = keep.tile([P, 4, C], BF16, name="vec_rows")
+        nc.vector.memset(vec_rows[:].rearrange("p v c -> p (v c)").bitcast(I32), 0)
+        one_col = keep.tile([P, 1], F32, name="one_col")
+        nc.vector.memset(one_col[:], 1.0)
+        eps_col = keep.tile([P, 1], F32, name="eps_col")
+        nc.vector.memset(eps_col[:], EPS)
+        ones_sq = keep.tile([P, P], BF16, name="ones_sq")
+        nc.vector.memset(ones_sq[:], 1.0)
+        warm = keep.tile([P, 1], F32, name="warm")
+        nc.scalar.activation(out=warm[:], in_=one_col[:], func=ACT.Sqrt)
+        vectors = (ln_w, ln_b, b2, b1)
+        for v, vec in enumerate(vectors):
+            nc.scalar.dma_start(out=vec_rows[0:1, v, 0 : vec.shape[0]], in_=vec.rearrange("(o c) -> o c", o=1))
+        ident = keep.tile([P, P], F32, name="ident")
+        make_identity(nc, ident[:])
+
+        weights = []
+        for name, words_dram, scales_dram in (("w1", W1_words, W1_scales), ("w2", W2_words, W2_scales)):
+            words = keep.tile([P, 4 * C], U8, name=name + "_words", align_bytes=64)
+            plane = keep.tile([P, C], U8, name=name + "_plane", align_bytes=64)
+            nc.vector.memset(plane[:].bitcast(I32), 0)
+            nc.sync.dma_start(out=words[:].bitcast(I32), in_=words_dram[0].rearrange("p n t -> p (n t)").bitcast(I32))
+            for quad in range(4):
+                nc.sync.dma_start(
+                    out=plane[32 * quad : 32 * quad + 4, :].bitcast(I32),
+                    in_=scales_dram[0, 4 * quad : 4 * quad + 4, :].bitcast(I32),
+                )
+            weights.append((words, plane))
+
+        lnw_bc = psum_ln.tile([P, C], F32, name="lnw_bc")
+        lnb_bc = psum_ln.tile([P, C], F32, name="lnb_bc")
+        b2_ps = psum_mm.tile([P, C], F32, name="b2_ps", tag="acc")
+        b1_ps = psum_mm.tile([P, C], F32, name="b1_ps", tag="acc")
+        for v, spread in enumerate((lnw_bc, lnb_bc, b2_ps, b1_ps)):
             nc.tensor.matmul(out=spread[:], lhsT=ones_sq[:], rhs=vec_rows[:, v, :], start=True, stop=True)
-            nc.scalar.copy(out=vec_bc[:, v, 0:width], in_=spread[:, 0:width])
-        lnw_bc = vec_bc[:, 0, 0:S]
-        lnb_bc = vec_bc[:, 1, 0:S]
-        b1_bc = vec_bc[:, 2, :]
-        b2_bc = vec_bc[:, 3, :]
 
         bn = keep.tile([P, 2, TILES, 6], F32, name="bn")
         mean_var = keep.tile([P, 2, TILES, 2], F32, name="mean_var")
-        for i in range(TILES):
-            nc.vector.bn_stats(out=bn[:, 0, i, :], in_=x_s[:, i, :])
-            nc.vector.bn_stats(out=bn[:, 1, i, :], in_=x_e[:, i, 0:M0])
-        for i in range(TILES):
-            nc.vector.bn_aggr(out=mean_var[:, 0, i, :], in_=bn[:, 0, i, :])
-            nc.vector.bn_aggr(out=mean_var[:, 1, i, :], in_=bn[:, 1, i, :])
         squares = keep.tile([P, TILES, ED - E1], F32, name="squares")
         square_sum = keep.tile([P, 2, TILES], F32, name="square_sum")
         for i in range(TILES):
+            nc.vector.bn_stats(out=bn[:, 0, i, :], in_=x_s[:, i, :])
+            nc.vector.bn_stats(out=bn[:, 1, i, :], in_=x_e[:, i, 0:M0])
             nc.scalar.activation(
                 out=squares[:, i, 0 : E2 - E1], in_=x_e[:, i, E1:E2], func=ACT.Square,
                 scale=D1**-0.25, accum_out=square_sum[:, 0, i : i + 1],
@@ -135,13 +105,26 @@ def tile_interactionblock_kernel(
                 out=squares[:, i, E2 - E1 :], in_=x_e[:, i, E2:ED], func=ACT.Square,
                 scale=D2**-0.25, accum_out=square_sum[:, 1, i : i + 1],
             )
+        for i in range(TILES):
+            nc.vector.bn_aggr(out=mean_var[:, 0, i, :], in_=bn[:, 0, i, :])
+            nc.vector.bn_aggr(out=mean_var[:, 1, i, :], in_=bn[:, 1, i, :])
         std = keep.tile([P, 4, TILES], F32, name="std")
-        nc.scalar.activation(out=std[:, 0:2, :], in_=mean_var[:, :, :, 1], func=ACT.Sqrt, bias=eps_col[:])
         nc.scalar.activation(
             out=std[:, 2, :], in_=square_sum[:, 0, :], func=ACT.Sqrt, scale=math.sqrt(D1) / M1, bias=eps_col[:]
         )
         nc.scalar.activation(
             out=std[:, 3, :], in_=square_sum[:, 1, :], func=ACT.Sqrt, scale=math.sqrt(D2) / M2, bias=eps_col[:]
+        )
+        nc.scalar.activation(out=std[:, 0:2, :], in_=mean_var[:, :, :, 1], func=ACT.Sqrt, bias=eps_col[:])
+        nc.scalar.activation(out=warm[:], in_=one_col[:], func=ACT.Silu)
+        norms = keep.tile([P, TILES, M1 + M2], F32, name="norms")
+        nc.vector.tensor_reduce(
+            out=norms[:, :, 0:M1], in_=squares[:, :, 0 : E2 - E1].rearrange("p i (c d) -> p i c d", d=D1),
+            axis=AXIS.X, op=ALU.add,
+        )
+        nc.vector.tensor_reduce(
+            out=norms[:, :, M1:], in_=squares[:, :, E2 - E1 :].rearrange("p i (c d) -> p i c d", d=D2),
+            axis=AXIS.X, op=ALU.add,
         )
         rstd = keep.tile([P, 4, TILES], F32, name="rstd")
         nc.vector.reciprocal(out=rstd[:], in_=std[:])
@@ -152,112 +135,161 @@ def tile_interactionblock_kernel(
         rvar = keep.tile([P, 2, TILES], F32, name="rvar")
         nc.vector.tensor_tensor(out=rvar[:], in0=rstd[:, 2:4, :], in1=rstd[:, 2:4, :], op=ALU.mult)
 
+        b2_bc = keep.tile([P, C], F32, name="b2_bc")
+        nc.scalar.copy(out=b2_bc[:], in_=b2_ps[:])
+        b1_bc = keep.tile([P, C], F32, name="b1_bc")
+        nc.scalar.copy(out=b1_bc[:], in_=b1_ps[:])
         xs_b2 = keep.tile([P, TILES, S], F32, name="xs_b2")
-        nc.gpsimd.tensor_tensor(
-            out=xs_b2[:], in0=x_s[:], in1=b2_bc[:, 0:S].unsqueeze(1).to_broadcast([P, TILES, S]), op=ALU.add
-        )
+        half_tiles = TILES // 2
+        for lo in (0, half_tiles):
+            nc.gpsimd.tensor_tensor(
+                out=xs_b2[:, lo : lo + half_tiles, :], in0=x_s[:, lo : lo + half_tiles, :],
+                in1=b2_bc[:, 0:S].unsqueeze(1).to_broadcast([P, half_tiles, S]), op=ALU.add,
+            )
 
         cat = keep.tile([P, TILES, C], BF16, name="cat", align_bytes=64)
-        for i in range(TILES):
-            centred = work.tile([P, S], F32, name="centred")
-            nc.vector.scalar_tensor_tensor(
-                out=centred[:], in0=x_s[:, i, :], scalar=mean_var[:, 0, i, 0:1], in1=lnw_bc,
-                op0=ALU.subtract, op1=ALU.mult,
-            )
-            nc.vector.scalar_tensor_tensor(
-                out=cat[:, i, 0:S], in0=centred[:], scalar=rstd[:, 0, i : i + 1], in1=lnb_bc,
-                op0=ALU.mult, op1=ALU.add,
-            )
-            nc.scalar.activation(
-                out=cat[:, i, S : S + M0], in_=x_e[:, i, 0:M0], func=ACT.Square,
-                scale=rstd[:, 1, i : i + 1], bias=shift0[:, i : i + 1],
-            )
-        norms = keep.tile([P, TILES, M1 + M2], F32, name="norms")
-        nc.vector.tensor_reduce(
-            out=norms[:, :, 0:M1], in_=squares[:, :, 0 : E2 - E1].rearrange("p i (c d) -> p i c d", d=D1),
-            axis=AXIS.X, op=ALU.add,
-        )
-        nc.vector.tensor_reduce(
-            out=norms[:, :, M1:], in_=squares[:, :, E2 - E1 :].rearrange("p i (c d) -> p i c d", d=D2),
-            axis=AXIS.X, op=ALU.add,
-        )
-        nc.vector.tensor_tensor(
-            out=cat[:, :, S + M0 : S + M0 + M1], in0=norms[:, :, 0:M1],
-            in1=rvar[:, 0, :].unsqueeze(2).to_broadcast([P, TILES, M1]), op=ALU.mult,
-        )
-        nc.vector.tensor_tensor(
-            out=cat[:, :, S + M0 + M1 :], in0=norms[:, :, M1:],
-            in1=rvar[:, 1, :].unsqueeze(2).to_broadcast([P, TILES, M2]), op=ALU.mult,
-        )
-
-        blocks = ((0, M0, 1), (M0, M0 + M1, 2), (M0 + M1, NI, 3))
+        hidden = keep.tile([P, TILES, C], BF16, name="hidden", align_bytes=64)
         gate_bias = keep.tile([P, TILES, NI], F32, name="gate_bias")
-        for i in range(TILES):
-            for lo, hi, kind in blocks:
-                nc.scalar.activation(
-                    out=gate_bias[:, i, lo:hi], in_=b2_bc[:, S + lo : S + hi], func=ACT.Identity,
-                    scale=rstd[:, kind, i : i + 1], bias=one_col[:],
-                )
-
         codes = keep.tile([P, 2, PAIRS, 2 * P], U32, name="codes", align_bytes=64)
         planes = keep.tile([P, 2, PAIRS, 2 * P], U8, name="planes", align_bytes=64)
-        hidden = keep.tile([P, TILES, C], BF16, name="hidden", align_bytes=64)
-        for pair in range(PAIRS):
-            transpose_and_quantise(nc, work, psum_t, ident, cat, pair, codes[:, 0, pair, :], planes[:, 0, pair, :])
-            for half in range(2):
-                i = 2 * pair + half
-                acc = psum_mm.tile([P, C], F32, name="acc")
-                nc.tensor.matmul_mx(
-                    out=acc[:],
-                    lhsT=codes[:, 0, pair, half * P : (half + 1) * P].bitcast(FP8X4),
-                    lhsT_scale=planes[:, 0, pair, half * P : (half + 1) * P],
-                    rhs=w1_words[:].bitcast(FP8X4),
-                    rhs_scale=w1_plane[:],
-                    start=True,
-                    stop=True,
-                )
-                biased = work.tile([P, C], F32, name="biased")
-                nc.vector.tensor_tensor(out=biased[:], in0=acc[:], in1=b1_bc, op=ALU.add)
-                nc.scalar.activation(out=hidden[:, i, :], in_=biased[:], func=ACT.Silu)
-
         res = keep.tile([P, TILES, S + ED], F32, name="res")
-        for pair in range(PAIRS):
-            transpose_and_quantise(nc, work, psum_t, ident, hidden, pair, codes[:, 1, pair, :], planes[:, 1, pair, :])
-            for half in range(2):
-                i = 2 * pair + half
+        blocks = ((0, M0, 1), (M0, M0 + M1, 2), (M0 + M1, NI, 3))
+        turned_of = {}
+        grouped_of = {}
+        acc_of = {}
+
+        def both(pair):
+            return (2 * pair, 2 * pair + 1)
+
+        def turn(src, layer, pair):
+            turned = psum_t.tile([P, 2, 2 * P], F32, name="turned")
+            for half, i in enumerate(both(pair)):
+                words = src[:, i, :].bitcast(F32)
+                for u in range(2):
+                    nc.tensor.transpose(turned[:, u, half * P : (half + 1) * P], words[:, u : C // 2 : 2], ident[:])
+            turned_of[(layer, pair)] = turned
+
+        def copy_out(layer, pair):
+            grouped = work.tile([P, 2 * P, 4], BF16, name="grouped", align_bytes=64)
+            nc.scalar.copy(
+                out=grouped[:].rearrange("p r t -> p (r t)").bitcast(F32).rearrange("p (r u) -> p r u", u=2),
+                in_=turned_of[(layer, pair)][:].rearrange("p u r -> p r u"),
+            )
+            grouped_of[(layer, pair)] = grouped
+
+        def quantise_and_multiply(layer, pair):
+            nc.vector.quantize_mx(
+                out=codes[:, layer, pair, :].bitcast(FP8X4),
+                scales=planes[:, layer, pair, :],
+                in_=grouped_of[(layer, pair)][:].rearrange("p r t -> p (r t)"),
+            )
+            w_words, w_plane = weights[layer]
+            for half, i in enumerate(both(pair)):
                 acc = psum_mm.tile([P, C], F32, name="acc")
                 nc.tensor.matmul_mx(
                     out=acc[:],
-                    lhsT=codes[:, 1, pair, half * P : (half + 1) * P].bitcast(FP8X4),
-                    lhsT_scale=planes[:, 1, pair, half * P : (half + 1) * P],
-                    rhs=w2_words[:].bitcast(FP8X4),
-                    rhs_scale=w2_plane[:],
+                    lhsT=codes[:, layer, pair, half * P : (half + 1) * P].bitcast(FP8X4),
+                    lhsT_scale=planes[:, layer, pair, half * P : (half + 1) * P],
+                    rhs=w_words[:].bitcast(FP8X4),
+                    rhs_scale=w_plane[:],
                     start=True,
                     stop=True,
                 )
-                nc.vector.tensor_tensor(out=res[:, i, 0:S], in0=acc[:, 0:S], in1=xs_b2[:, i, :], op=ALU.add)
-                factor = work.tile([P, NI], F32, name="factor")
+                acc_of[(layer, i)] = acc
+
+        def invariants(pair):
+            for i in both(pair):
+                nc.scalar.activation(
+                    out=cat[:, i, S : S + M0], in_=x_e[:, i, 0:M0], func=ACT.Square,
+                    scale=rstd[:, 1, i : i + 1], bias=shift0[:, i : i + 1],
+                )
+                nc.scalar.activation(
+                    out=cat[:, i, S + M0 : S + M0 + M1], in_=norms[:, i, 0:M1], func=ACT.Copy,
+                    scale=rvar[:, 0, i : i + 1],
+                )
+                nc.scalar.activation(
+                    out=cat[:, i, S + M0 + M1 :], in_=norms[:, i, M1:], func=ACT.Copy,
+                    scale=rvar[:, 1, i : i + 1],
+                )
+
+        def layer_norm(pair):
+            centred = {}
+            for i in both(pair):
+                centred[i] = work.tile([P, S], F32, name="centred")
+                nc.vector.scalar_tensor_tensor(
+                    out=centred[i][:], in0=x_s[:, i, :], scalar=mean_var[:, 0, i, 0:1], in1=lnw_bc[:, 0:S],
+                    op0=ALU.subtract, op1=ALU.mult,
+                )
+            for i in both(pair):
+                nc.vector.scalar_tensor_tensor(
+                    out=cat[:, i, 0:S], in0=centred[i][:], scalar=rstd[:, 0, i : i + 1], in1=lnb_bc[:, 0:S],
+                    op0=ALU.mult, op1=ALU.add,
+                )
+            turn(cat, 0, pair)
+
+        def copy_out_cat(pair):
+            copy_out(0, pair)
+            for i in both(pair):
+                for lo, hi, kind in blocks:
+                    nc.scalar.activation(
+                        out=gate_bias[:, i, lo:hi], in_=b2_bc[:, S + lo : S + hi], func=ACT.Identity,
+                        scale=rstd[:, kind, i : i + 1], bias=one_col[:],
+                    )
+
+        def first_layer(pair):
+            quantise_and_multiply(0, pair)
+
+        def activate(pair):
+            for i in both(pair):
+                biased = work.tile([P, C], F32, name="biased")
+                nc.vector.tensor_tensor(out=biased[:], in0=acc_of[(0, i)][:], in1=b1_bc[:], op=ALU.add)
+                nc.scalar.activation(out=hidden[:, i, :], in_=biased[:], func=ACT.Silu)
+            turn(hidden, 1, pair)
+
+        def copy_out_hidden(pair):
+            copy_out(1, pair)
+
+        def second_layer(pair):
+            quantise_and_multiply(1, pair)
+
+        def gate_and_add(pair):
+            factor = {}
+            for i in both(pair):
+                factor[i] = work.tile([P, NI], F32, name="factor")
                 for lo, hi, kind in blocks:
                     nc.vector.scalar_tensor_tensor(
-                        out=factor[:, lo:hi], in0=acc[:, S + lo : S + hi], scalar=rstd[:, kind, i : i + 1],
-                        in1=gate_bias[:, i, lo:hi], op0=ALU.mult, op1=ALU.add,
+                        out=factor[i][:, lo:hi], in0=acc_of[(1, i)][:, S + lo : S + hi],
+                        scalar=rstd[:, kind, i : i + 1], in1=gate_bias[:, i, lo:hi], op0=ALU.mult, op1=ALU.add,
                     )
-                mean0 = mean_var[:, 1, i, 0:1]
+            for i in both(pair):
+                nc.vector.tensor_tensor(out=res[:, i, 0:S], in0=acc_of[(1, i)][:, 0:S], in1=xs_b2[:, i, :], op=ALU.add)
+            for i in both(pair):
                 nc.vector.scalar_tensor_tensor(
-                    out=res[:, i, S : S + M0], in0=x_e[:, i, 0:M0], scalar=mean0, in1=factor[:, 0:M0],
-                    op0=ALU.subtract, op1=ALU.mult,
+                    out=res[:, i, S : S + M0], in0=x_e[:, i, 0:M0], scalar=mean_var[:, 1, i, 0:1],
+                    in1=factor[i][:, 0:M0], op0=ALU.subtract, op1=ALU.mult,
                 )
                 nc.vector.tensor_tensor(
                     out=res[:, i, S + E1 : S + E2].rearrange("p (c d) -> p c d", d=D1),
                     in0=x_e[:, i, E1:E2].rearrange("p (c d) -> p c d", d=D1),
-                    in1=factor[:, M0 : M0 + M1].unsqueeze(2).to_broadcast([P, M1, D1]),
+                    in1=factor[i][:, M0 : M0 + M1].unsqueeze(2).to_broadcast([P, M1, D1]),
                     op=ALU.mult,
                 )
                 nc.vector.tensor_tensor(
                     out=res[:, i, S + E2 :].rearrange("p (c d) -> p c d", d=D2),
                     in0=x_e[:, i, E2:ED].rearrange("p (c d) -> p c d", d=D2),
-                    in1=factor[:, M0 + M1 :].unsqueeze(2).to_broadcast([P, M2, D2]),
+                    in1=factor[i][:, M0 + M1 :].unsqueeze(2).to_broadcast([P, M2, D2]),
                     op=ALU.mult,
                 )
-                nc.vector.tensor_scalar_add(out=res[:, i, S : S + M0], in0=res[:, i, S : S + M0], scalar1=mean0)
+            for i in both(pair):
+                nc.vector.tensor_scalar_add(
+                    out=res[:, i, S : S + M0], in0=res[:, i, S : S + M0], scalar1=mean_var[:, 1, i, 0:1]
+                )
                 nc.sync.dma_start(out=out_dram[:, i, :], in_=res[:, i, :])
+
+        stages = (
+            invariants, layer_norm, copy_out_cat, first_layer, activate, copy_out_hidden, second_layer, gate_and_add
+        )
+        for step in range(PAIRS + len(stages) - 1):
+            for lag, stage in enumerate(stages):
+                if 0 <= step - lag < PAIRS:
+                    stage(step - lag)

@@ -94,20 +94,41 @@ def tile_interactionblock_kernel(
         mean_var = keep.tile([P, 2, TILES, 2], F32, name="mean_var")
         squares = keep.tile([P, TILES, ED - E1], F32, name="squares")
         square_sum = keep.tile([P, 2, TILES], F32, name="square_sum")
-        for i in range(TILES):
-            nc.vector.bn_stats(out=bn[:, 0, i, :], in_=x_s[:, i, :])
-            nc.vector.bn_stats(out=bn[:, 1, i, :], in_=x_e[:, i, 0:M0])
-            nc.scalar.activation(
-                out=squares[:, i, 0 : E2 - E1], in_=x_e[:, i, E1:E2], func=ACT.Square,
-                scale=D1**-0.25, accum_out=square_sum[:, 0, i : i + 1],
+        norms = keep.tile([P, TILES, M1 + M2], F32, name="norms")
+        part1 = keep.tile([P, TILES, M1], F32, name="part1")
+        part2 = keep.tile([P, TILES, M2, 2], F32, name="part2")
+        half_tiles = TILES // 2
+        for lo in (0, half_tiles):
+            for i in range(lo, lo + half_tiles):
+                nc.vector.bn_stats(out=bn[:, 0, i, :], in_=x_s[:, i, :])
+                nc.vector.bn_stats(out=bn[:, 1, i, :], in_=x_e[:, i, 0:M0])
+                nc.scalar.activation(
+                    out=squares[:, i, 0 : E2 - E1], in_=x_e[:, i, E1:E2], func=ACT.Square,
+                    scale=D1**-0.25, accum_out=square_sum[:, 0, i : i + 1],
+                )
+                nc.scalar.activation(
+                    out=squares[:, i, E2 - E1 :], in_=x_e[:, i, E2:ED], func=ACT.Square,
+                    scale=D2**-0.25, accum_out=square_sum[:, 1, i : i + 1],
+                )
+            four = slice(lo, lo + half_tiles)
+            sq1 = squares[:, four, 0 : E2 - E1].rearrange("p i (c d) -> p i c d", d=D1)
+            sq2 = squares[:, four, E2 - E1 :].rearrange("p i (c d) -> p i c d", d=D2)
+            nc.gpsimd.tensor_tensor(out=part1[:, four, :], in0=sq1[:, :, :, 0], in1=sq1[:, :, :, 1], op=ALU.add)
+            nc.gpsimd.tensor_tensor(out=part2[:, four, :, :], in0=sq2[:, :, :, 0:2], in1=sq2[:, :, :, 2:4], op=ALU.add)
+            nc.gpsimd.tensor_tensor(out=norms[:, four, 0:M1], in0=part1[:, four, :], in1=sq1[:, :, :, 2], op=ALU.add)
+            nc.gpsimd.tensor_tensor(
+                out=part2[:, four, :, 0], in0=part2[:, four, :, 0], in1=part2[:, four, :, 1], op=ALU.add
             )
-            nc.scalar.activation(
-                out=squares[:, i, E2 - E1 :], in_=x_e[:, i, E2:ED], func=ACT.Square,
-                scale=D2**-0.25, accum_out=square_sum[:, 1, i : i + 1],
-            )
+            nc.gpsimd.tensor_tensor(out=norms[:, four, M1:], in0=part2[:, four, :, 0], in1=sq2[:, :, :, 4], op=ALU.add)
         for i in range(TILES):
             nc.vector.bn_aggr(out=mean_var[:, 0, i, :], in_=bn[:, 0, i, :])
             nc.vector.bn_aggr(out=mean_var[:, 1, i, :], in_=bn[:, 1, i, :])
+        centred = keep.tile([P, TILES, S], F32, name="centred")
+        for i in range(TILES):
+            nc.vector.scalar_tensor_tensor(
+                out=centred[:, i, :], in0=x_s[:, i, :], scalar=mean_var[:, 0, i, 0:1], in1=lnw_bc[:, 0:S],
+                op0=ALU.subtract, op1=ALU.mult,
+            )
         std = keep.tile([P, 4, TILES], F32, name="std")
         nc.scalar.activation(
             out=std[:, 2, :], in_=square_sum[:, 0, :], func=ACT.Sqrt, scale=math.sqrt(D1) / M1, bias=eps_col[:]
@@ -117,15 +138,6 @@ def tile_interactionblock_kernel(
         )
         nc.scalar.activation(out=std[:, 0:2, :], in_=mean_var[:, :, :, 1], func=ACT.Sqrt, bias=eps_col[:])
         nc.scalar.activation(out=warm[:], in_=one_col[:], func=ACT.Silu)
-        norms = keep.tile([P, TILES, M1 + M2], F32, name="norms")
-        nc.vector.tensor_reduce(
-            out=norms[:, :, 0:M1], in_=squares[:, :, 0 : E2 - E1].rearrange("p i (c d) -> p i c d", d=D1),
-            axis=AXIS.X, op=ALU.add,
-        )
-        nc.vector.tensor_reduce(
-            out=norms[:, :, M1:], in_=squares[:, :, E2 - E1 :].rearrange("p i (c d) -> p i c d", d=D2),
-            axis=AXIS.X, op=ALU.add,
-        )
         rstd = keep.tile([P, 4, TILES], F32, name="rstd")
         nc.vector.reciprocal(out=rstd[:], in_=std[:])
         shift0 = keep.tile([P, TILES], F32, name="shift0")
@@ -140,7 +152,6 @@ def tile_interactionblock_kernel(
         b1_bc = keep.tile([P, C], F32, name="b1_bc")
         nc.scalar.copy(out=b1_bc[:], in_=b1_ps[:])
         xs_b2 = keep.tile([P, TILES, S], F32, name="xs_b2")
-        half_tiles = TILES // 2
         for lo in (0, half_tiles):
             nc.gpsimd.tensor_tensor(
                 out=xs_b2[:, lo : lo + half_tiles, :], in0=x_s[:, lo : lo + half_tiles, :],
@@ -213,16 +224,9 @@ def tile_interactionblock_kernel(
                 )
 
         def layer_norm(pair):
-            centred = {}
-            for i in both(pair):
-                centred[i] = work.tile([P, S], F32, name="centred")
-                nc.vector.scalar_tensor_tensor(
-                    out=centred[i][:], in0=x_s[:, i, :], scalar=mean_var[:, 0, i, 0:1], in1=lnw_bc[:, 0:S],
-                    op0=ALU.subtract, op1=ALU.mult,
-                )
             for i in both(pair):
                 nc.vector.scalar_tensor_tensor(
-                    out=cat[:, i, 0:S], in0=centred[i][:], scalar=rstd[:, 0, i : i + 1], in1=lnb_bc[:, 0:S],
+                    out=cat[:, i, 0:S], in0=centred[:, i, :], scalar=rstd[:, 0, i : i + 1], in1=lnb_bc[:, 0:S],
                     op0=ALU.mult, op1=ALU.add,
                 )
             turn(cat, 0, pair)
@@ -268,6 +272,11 @@ def tile_interactionblock_kernel(
                     out=res[:, i, S : S + M0], in0=x_e[:, i, 0:M0], scalar=mean_var[:, 1, i, 0:1],
                     in1=factor[i][:, 0:M0], op0=ALU.subtract, op1=ALU.mult,
                 )
+                nc.scalar.activation(
+                    out=res[:, i, S : S + M0], in_=res[:, i, S : S + M0], func=ACT.Identity,
+                    bias=mean_var[:, 1, i, 0:1],
+                )
+            for i in both(pair):
                 nc.vector.tensor_tensor(
                     out=res[:, i, S + E1 : S + E2].rearrange("p (c d) -> p c d", d=D1),
                     in0=x_e[:, i, E1:E2].rearrange("p (c d) -> p c d", d=D1),
@@ -279,10 +288,6 @@ def tile_interactionblock_kernel(
                     in0=x_e[:, i, E2:ED].rearrange("p (c d) -> p c d", d=D2),
                     in1=factor[i][:, M0 + M1 :].unsqueeze(2).to_broadcast([P, M2, D2]),
                     op=ALU.mult,
-                )
-            for i in both(pair):
-                nc.vector.tensor_scalar_add(
-                    out=res[:, i, S : S + M0], in0=res[:, i, S : S + M0], scalar1=mean_var[:, 1, i, 0:1]
                 )
                 nc.sync.dma_start(out=out_dram[:, i, :], in_=res[:, i, :])
 

@@ -152,18 +152,16 @@ def tile_interactionblock_kernel(
         b1_bc = keep.tile([P, C], F32, name="b1_bc")
         nc.scalar.copy(out=b1_bc[:], in_=b1_ps[:])
         xs_b2 = keep.tile([P, TILES, S], F32, name="xs_b2")
-        for lo in (0, half_tiles):
-            nc.gpsimd.tensor_tensor(
-                out=xs_b2[:, lo : lo + half_tiles, :], in0=x_s[:, lo : lo + half_tiles, :],
-                in1=b2_bc[:, 0:S].unsqueeze(1).to_broadcast([P, half_tiles, S]), op=ALU.add,
-            )
+        for i in range(TILES):
+            nc.gpsimd.tensor_tensor(out=xs_b2[:, i, :], in0=x_s[:, i, :], in1=b2_bc[:, 0:S], op=ALU.add)
 
         cat = keep.tile([P, TILES, C], BF16, name="cat", align_bytes=64)
         hidden = keep.tile([P, TILES, C], BF16, name="hidden", align_bytes=64)
         gate_bias = keep.tile([P, TILES, NI], F32, name="gate_bias")
         codes = keep.tile([P, 2, PAIRS, 2 * P], U32, name="codes", align_bytes=64)
         planes = keep.tile([P, 2, PAIRS, 2 * P], U8, name="planes", align_bytes=64)
-        res = keep.tile([P, TILES, S + ED], F32, name="res")
+        res_s = keep.tile([P, TILES, S], F32, name="res_s")
+        res_e = keep.tile([P, TILES, ED], F32, name="res_e")
         blocks = ((0, M0, 1), (M0, M0 + M1, 2), (M0 + M1, NI, 3))
         turned_of = {}
         grouped_of = {}
@@ -233,12 +231,6 @@ def tile_interactionblock_kernel(
 
         def copy_out_cat(pair):
             copy_out(0, pair)
-            for i in both(pair):
-                for lo, hi, kind in blocks:
-                    nc.scalar.activation(
-                        out=gate_bias[:, i, lo:hi], in_=b2_bc[:, S + lo : S + hi], func=ACT.Identity,
-                        scale=rstd[:, kind, i : i + 1], bias=one_col[:],
-                    )
 
         def first_layer(pair):
             quantise_and_multiply(0, pair)
@@ -255,6 +247,12 @@ def tile_interactionblock_kernel(
 
         def second_layer(pair):
             quantise_and_multiply(1, pair)
+            for i in both(pair):
+                for lo, hi, kind in blocks:
+                    nc.scalar.activation(
+                        out=gate_bias[:, i, lo:hi], in_=b2_bc[:, S + lo : S + hi], func=ACT.Identity,
+                        scale=rstd[:, kind, i : i + 1], bias=one_col[:],
+                    )
 
         def gate_and_add(pair):
             factor = {}
@@ -266,30 +264,31 @@ def tile_interactionblock_kernel(
                         scalar=rstd[:, kind, i : i + 1], in1=gate_bias[:, i, lo:hi], op0=ALU.mult, op1=ALU.add,
                     )
             for i in both(pair):
-                nc.vector.tensor_tensor(out=res[:, i, 0:S], in0=acc_of[(1, i)][:, 0:S], in1=xs_b2[:, i, :], op=ALU.add)
+                nc.vector.tensor_tensor(out=res_s[:, i, :], in0=acc_of[(1, i)][:, 0:S], in1=xs_b2[:, i, :], op=ALU.add)
+                nc.sync.dma_start(out=out_dram[:, i, 0:S], in_=res_s[:, i, :])
             for i in both(pair):
                 nc.vector.scalar_tensor_tensor(
-                    out=res[:, i, S : S + M0], in0=x_e[:, i, 0:M0], scalar=mean_var[:, 1, i, 0:1],
+                    out=res_e[:, i, 0:M0], in0=x_e[:, i, 0:M0], scalar=mean_var[:, 1, i, 0:1],
                     in1=factor[i][:, 0:M0], op0=ALU.subtract, op1=ALU.mult,
                 )
                 nc.scalar.activation(
-                    out=res[:, i, S : S + M0], in_=res[:, i, S : S + M0], func=ACT.Identity,
+                    out=res_e[:, i, 0:M0], in_=res_e[:, i, 0:M0], func=ACT.Identity,
                     bias=mean_var[:, 1, i, 0:1],
                 )
             for i in both(pair):
                 nc.vector.tensor_tensor(
-                    out=res[:, i, S + E1 : S + E2].rearrange("p (c d) -> p c d", d=D1),
+                    out=res_e[:, i, E1:E2].rearrange("p (c d) -> p c d", d=D1),
                     in0=x_e[:, i, E1:E2].rearrange("p (c d) -> p c d", d=D1),
                     in1=factor[i][:, M0 : M0 + M1].unsqueeze(2).to_broadcast([P, M1, D1]),
                     op=ALU.mult,
                 )
                 nc.vector.tensor_tensor(
-                    out=res[:, i, S + E2 :].rearrange("p (c d) -> p c d", d=D2),
+                    out=res_e[:, i, E2:ED].rearrange("p (c d) -> p c d", d=D2),
                     in0=x_e[:, i, E2:ED].rearrange("p (c d) -> p c d", d=D2),
                     in1=factor[i][:, M0 + M1 :].unsqueeze(2).to_broadcast([P, M2, D2]),
                     op=ALU.mult,
                 )
-                nc.sync.dma_start(out=out_dram[:, i, :], in_=res[:, i, :])
+                nc.sync.dma_start(out=out_dram[:, i, S:], in_=res_e[:, i, :])
 
         stages = (
             invariants, layer_norm, copy_out_cat, first_layer, activate, copy_out_hidden, second_layer, gate_and_add

@@ -44,7 +44,7 @@ def tile_interactionblock_kernel(
         work = ctx.enter_context(tc.tile_pool(name="work", bufs=3))
         psum_ln = ctx.enter_context(tc.psum_pool(name="psum_ln", bufs=1))
         psum_t = ctx.enter_context(tc.psum_pool(name="psum_t", bufs=2))
-        psum_mm = ctx.enter_context(tc.psum_pool(name="psum_mm", bufs=4))
+        psum_mm = ctx.enter_context(tc.psum_pool(name="psum_mm", bufs=2))
         ctx.enter_context(tc.manual_schedule())
 
         x_s = keep.tile([P, TILES, S], BF16, name="x_s")
@@ -54,7 +54,7 @@ def tile_interactionblock_kernel(
             nc.sync.dma_start(out=x_s[:, two, :], in_=xs_dram[:, two, :])
             nc.sync.dma_start(out=x_e[:, two, :], in_=xe_dram[:, two, :])
 
-        vec_rows = keep.tile([P, 4, C], BF16, name="vec_rows")
+        vec_rows = keep.tile([P, 3, C], BF16, name="vec_rows")
         nc.vector.memset(vec_rows[:].rearrange("p v c -> p (v c)").bitcast(I32), 0)
         one_col = keep.tile([P, 1], F32, name="one_col")
         nc.vector.memset(one_col[:], 1.0)
@@ -64,9 +64,11 @@ def tile_interactionblock_kernel(
         nc.vector.memset(ones_sq[:], 1.0)
         warm = keep.tile([P, 1], F32, name="warm")
         nc.scalar.activation(out=warm[:], in_=one_col[:], func=ACT.Sqrt)
-        vectors = (ln_w, ln_b, b2, b1)
+        vectors = (ln_w, ln_b, b2)
         for v, vec in enumerate(vectors):
             nc.scalar.dma_start(out=vec_rows[0:1, v, 0 : vec.shape[0]], in_=vec.rearrange("(o c) -> o c", o=1))
+        b1_col = keep.tile([P, 4], BF16, name="b1_col")
+        nc.scalar.dma_start(out=b1_col[:], in_=b1.rearrange("(p t) -> p t", t=4))
         ident = keep.tile([P, P], F32, name="ident")
         make_identity(nc, ident[:])
 
@@ -86,8 +88,7 @@ def tile_interactionblock_kernel(
         lnw_bc = psum_ln.tile([P, C], F32, name="lnw_bc")
         lnb_bc = psum_ln.tile([P, C], F32, name="lnb_bc")
         b2_ps = psum_mm.tile([P, C], F32, name="b2_ps", tag="acc")
-        b1_ps = psum_mm.tile([P, C], F32, name="b1_ps", tag="acc")
-        for v, spread in enumerate((lnw_bc, lnb_bc, b2_ps, b1_ps)):
+        for v, spread in enumerate((lnw_bc, lnb_bc, b2_ps)):
             nc.tensor.matmul(out=spread[:], lhsT=ones_sq[:], rhs=vec_rows[:, v, :], start=True, stop=True)
 
         bn = keep.tile([P, 2, TILES, 6], F32, name="bn")
@@ -120,6 +121,17 @@ def tile_interactionblock_kernel(
                 out=part2[:, four, :, 0], in0=part2[:, four, :, 0], in1=part2[:, four, :, 1], op=ALU.add
             )
             nc.gpsimd.tensor_tensor(out=norms[:, four, M1:], in0=part2[:, four, :, 0], in1=sq2[:, :, :, 4], op=ALU.add)
+        w1_words, w1_plane = weights[0]
+        w1p_words = keep.tile([P, C], U32, name="w1p_words", align_bytes=64)
+        w1p_plane = keep.tile([P, C], U8, name="w1p_plane", align_bytes=64)
+        nc.vector.tensor_copy(
+            out=w1p_words[:].bitcast(I32).rearrange("p (t m) -> p t m", t=4),
+            in_=w1_words[:].bitcast(I32).rearrange("p (m t) -> p t m", t=4),
+        )
+        nc.vector.tensor_copy(
+            out=w1p_plane[:].rearrange("p (t m) -> p m t", t=4),
+            in_=w1_plane[:].rearrange("p (m t) -> p m t", t=4),
+        )
         for i in range(TILES):
             nc.vector.bn_aggr(out=mean_var[:, 0, i, :], in_=bn[:, 0, i, :])
             nc.vector.bn_aggr(out=mean_var[:, 1, i, :], in_=bn[:, 1, i, :])
@@ -149,23 +161,21 @@ def tile_interactionblock_kernel(
 
         b2_bc = keep.tile([P, C], F32, name="b2_bc")
         nc.scalar.copy(out=b2_bc[:], in_=b2_ps[:])
-        b1_bc = keep.tile([P, C], F32, name="b1_bc")
-        nc.scalar.copy(out=b1_bc[:], in_=b1_ps[:])
-        xs_b2 = keep.tile([P, TILES, S], F32, name="xs_b2")
+        addend = keep.tile([P, TILES, C], F32, name="addend")
         for i in range(TILES):
-            nc.gpsimd.tensor_tensor(out=xs_b2[:, i, :], in0=x_s[:, i, :], in1=b2_bc[:, 0:S], op=ALU.add)
+            nc.gpsimd.tensor_tensor(out=addend[:, i, 0:S], in0=x_s[:, i, :], in1=b2_bc[:, 0:S], op=ALU.add)
 
         cat = keep.tile([P, TILES, C], BF16, name="cat", align_bytes=64)
-        hidden = keep.tile([P, TILES, C], BF16, name="hidden", align_bytes=64)
-        gate_bias = keep.tile([P, TILES, NI], F32, name="gate_bias")
         codes = keep.tile([P, 2, PAIRS, 2 * P], U32, name="codes", align_bytes=64)
         planes = keep.tile([P, 2, PAIRS, 2 * P], U8, name="planes", align_bytes=64)
-        res_s = keep.tile([P, TILES, S], F32, name="res_s")
         res_e = keep.tile([P, TILES, ED], F32, name="res_e")
         blocks = ((0, M0, 1), (M0, M0 + M1, 2), (M0 + M1, NI, 3))
         turned_of = {}
         grouped_of = {}
         acc_of = {}
+        hid_of = {}
+        h_of = {}
+        hidden_of = {}
 
         def both(pair):
             return (2 * pair, 2 * pair + 1)
@@ -186,12 +196,32 @@ def tile_interactionblock_kernel(
             )
             grouped_of[(layer, pair)] = grouped
 
-        def quantise_and_multiply(layer, pair):
+        def quantise(layer, pair):
             nc.vector.quantize_mx(
                 out=codes[:, layer, pair, :].bitcast(FP8X4),
                 scales=planes[:, layer, pair, :],
                 in_=grouped_of[(layer, pair)][:].rearrange("p r t -> p (r t)"),
             )
+
+        def first_layer(pair):
+            quantise(0, pair)
+            for u in range(2):
+                hid = psum_mm.tile([P, 2, 2 * P], F32, name="hid")
+                for e in range(2):
+                    t = 2 * u + e
+                    nc.tensor.matmul_mx(
+                        out=hid[:, e, :],
+                        lhsT=w1p_words[:, t * P : (t + 1) * P].bitcast(FP8X4),
+                        lhsT_scale=w1p_plane[:, t * P : (t + 1) * P],
+                        rhs=codes[:, 0, pair, :].bitcast(FP8X4),
+                        rhs_scale=planes[:, 0, pair, :],
+                        start=True,
+                        stop=True,
+                    )
+                hid_of[(pair, u)] = hid
+
+        def quantise_and_multiply(layer, pair):
+            quantise(layer, pair)
             w_words, w_plane = weights[layer]
             for half, i in enumerate(both(pair)):
                 acc = psum_mm.tile([P, C], F32, name="acc")
@@ -232,61 +262,58 @@ def tile_interactionblock_kernel(
         def copy_out_cat(pair):
             copy_out(0, pair)
 
-        def first_layer(pair):
-            quantise_and_multiply(0, pair)
-
         def activate(pair):
-            for i in both(pair):
-                biased = work.tile([P, C], F32, name="biased")
-                nc.vector.tensor_tensor(out=biased[:], in0=acc_of[(0, i)][:], in1=b1_bc[:], op=ALU.add)
-                nc.scalar.activation(out=hidden[:, i, :], in_=biased[:], func=ACT.Silu)
-            turn(hidden, 1, pair)
+            hidden = work.tile([P, 4, 2 * P], BF16, name="hidden")
+            for t in range(4):
+                nc.scalar.activation(
+                    out=hidden[:, t, :], in_=hid_of[(pair, t // 2)][:, t % 2, :], func=ACT.Silu,
+                    bias=b1_col[:, t : t + 1],
+                )
+            hidden_of[pair] = hidden
 
         def copy_out_hidden(pair):
-            copy_out(1, pair)
+            grouped = work.tile([P, 2 * P, 4], BF16, name="grouped", align_bytes=64)
+            nc.vector.tensor_copy(out=grouped[:], in_=hidden_of[pair][:].rearrange("p t r -> p r t"))
+            grouped_of[(1, pair)] = grouped
 
         def second_layer(pair):
             quantise_and_multiply(1, pair)
             for i in both(pair):
                 for lo, hi, kind in blocks:
                     nc.scalar.activation(
-                        out=gate_bias[:, i, lo:hi], in_=b2_bc[:, S + lo : S + hi], func=ACT.Identity,
-                        scale=rstd[:, kind, i : i + 1], bias=one_col[:],
+                        out=addend[:, i, S + lo : S + hi], in_=b2_bc[:, S + lo : S + hi], func=ACT.Identity,
+                        bias=std[:, kind, i : i + 1],
                     )
 
         def gate_and_add(pair):
-            factor = {}
             for i in both(pair):
-                factor[i] = work.tile([P, NI], F32, name="factor")
-                for lo, hi, kind in blocks:
-                    nc.vector.scalar_tensor_tensor(
-                        out=factor[i][:, lo:hi], in0=acc_of[(1, i)][:, S + lo : S + hi],
-                        scalar=rstd[:, kind, i : i + 1], in1=gate_bias[:, i, lo:hi], op0=ALU.mult, op1=ALU.add,
-                    )
-            for i in both(pair):
-                nc.vector.tensor_tensor(out=res_s[:, i, :], in0=acc_of[(1, i)][:, 0:S], in1=xs_b2[:, i, :], op=ALU.add)
-                nc.sync.dma_start(out=out_dram[:, i, 0:S], in_=res_s[:, i, :])
+                h = keep.tile([P, C], F32, name="h%d" % i)
+                nc.vector.tensor_tensor(out=h[:], in0=acc_of[(1, i)][:], in1=addend[:, i, :], op=ALU.add)
+                nc.sync.dma_start(out=out_dram[:, i, 0:S], in_=h[:, 0:S])
+                h_of[i] = h
             for i in both(pair):
                 nc.vector.scalar_tensor_tensor(
                     out=res_e[:, i, 0:M0], in0=x_e[:, i, 0:M0], scalar=mean_var[:, 1, i, 0:1],
-                    in1=factor[i][:, 0:M0], op0=ALU.subtract, op1=ALU.mult,
+                    in1=h_of[i][:, S : S + M0], op0=ALU.subtract, op1=ALU.mult,
                 )
                 nc.scalar.activation(
                     out=res_e[:, i, 0:M0], in_=res_e[:, i, 0:M0], func=ACT.Identity,
-                    bias=mean_var[:, 1, i, 0:1],
+                    scale=rstd[:, 1, i : i + 1], bias=mean_var[:, 1, i, 0:1],
                 )
             for i in both(pair):
-                nc.vector.tensor_tensor(
+                nc.vector.scalar_tensor_tensor(
                     out=res_e[:, i, E1:E2].rearrange("p (c d) -> p c d", d=D1),
-                    in0=x_e[:, i, E1:E2].rearrange("p (c d) -> p c d", d=D1),
-                    in1=factor[i][:, M0 : M0 + M1].unsqueeze(2).to_broadcast([P, M1, D1]),
-                    op=ALU.mult,
+                    in0=h_of[i][:, S + M0 : S + M0 + M1].unsqueeze(2).to_broadcast([P, M1, D1]),
+                    scalar=rstd[:, 2, i : i + 1],
+                    in1=x_e[:, i, E1:E2].rearrange("p (c d) -> p c d", d=D1),
+                    op0=ALU.mult, op1=ALU.mult,
                 )
-                nc.vector.tensor_tensor(
+                nc.vector.scalar_tensor_tensor(
                     out=res_e[:, i, E2:ED].rearrange("p (c d) -> p c d", d=D2),
-                    in0=x_e[:, i, E2:ED].rearrange("p (c d) -> p c d", d=D2),
-                    in1=factor[i][:, M0 + M1 :].unsqueeze(2).to_broadcast([P, M2, D2]),
-                    op=ALU.mult,
+                    in0=h_of[i][:, S + M0 + M1 :].unsqueeze(2).to_broadcast([P, M2, D2]),
+                    scalar=rstd[:, 3, i : i + 1],
+                    in1=x_e[:, i, E2:ED].rearrange("p (c d) -> p c d", d=D2),
+                    op0=ALU.mult, op1=ALU.mult,
                 )
                 nc.sync.dma_start(out=out_dram[:, i, S:], in_=res_e[:, i, :])
 

@@ -12,7 +12,6 @@ U8 = mybir.dt.uint8
 FP8X4 = mybir.dt.float8_e4m3fn_x4
 ALU = mybir.AluOpType
 ACT = mybir.ActivationFunctionType
-AXIS = mybir.AxisListType
 
 P = 128
 ROWS = 1024
@@ -47,6 +46,9 @@ def tile_interactionblock_kernel(
         psum_mm = ctx.enter_context(tc.psum_pool(name="psum_mm", bufs=2))
         ctx.enter_context(tc.manual_schedule())
 
+        def both(pair):
+            return (2 * pair, 2 * pair + 1)
+
         x_s = keep.tile([P, TILES, S], BF16, name="x_s")
         x_e = keep.tile([P, TILES, ED], BF16, name="x_e")
         for pair in range(PAIRS):
@@ -58,10 +60,10 @@ def tile_interactionblock_kernel(
         nc.vector.memset(vec_rows[:].rearrange("p v c -> p (v c)").bitcast(I32), 0)
         one_col = keep.tile([P, 1], F32, name="one_col")
         nc.vector.memset(one_col[:], 1.0)
-        eps_col = keep.tile([P, 1], F32, name="eps_col")
-        nc.vector.memset(eps_col[:], EPS)
         ones_sq = keep.tile([P, P], BF16, name="ones_sq")
         nc.vector.memset(ones_sq[:], 1.0)
+        eps_col = keep.tile([P, 1], F32, name="eps_col")
+        nc.vector.memset(eps_col[:], EPS)
         warm = keep.tile([P, 1], F32, name="warm")
         nc.scalar.activation(out=warm[:], in_=one_col[:], func=ACT.Sqrt)
         vectors = (ln_w, ln_b, b2)
@@ -92,12 +94,23 @@ def tile_interactionblock_kernel(
             nc.tensor.matmul(out=spread[:], lhsT=ones_sq[:], rhs=vec_rows[:, v, :], start=True, stop=True)
 
         bn = keep.tile([P, 2, TILES, 6], F32, name="bn")
-        mean_var = keep.tile([P, 2, TILES, 2], F32, name="mean_var")
         squares = keep.tile([P, TILES, ED - E1], F32, name="squares")
         square_sum = keep.tile([P, 2, TILES], F32, name="square_sum")
         norms = keep.tile([P, TILES, M1 + M2], F32, name="norms")
         part1 = keep.tile([P, TILES, M1], F32, name="part1")
         part2 = keep.tile([P, TILES, M2, 2], F32, name="part2")
+
+        def component_sums(engine, first, last):
+            two = slice(first, last)
+            sq1 = squares[:, two, 0 : E2 - E1].rearrange("p i (c d) -> p i c d", d=D1)
+            sq2 = squares[:, two, E2 - E1 :].rearrange("p i (c d) -> p i c d", d=D2)
+            engine.tensor_tensor(out=part1[:, two, :], in0=sq1[:, :, :, 0], in1=sq1[:, :, :, 1], op=ALU.add)
+            engine.tensor_tensor(out=part2[:, two, :, :], in0=sq2[:, :, :, 0:2], in1=sq2[:, :, :, 2:4], op=ALU.add)
+            engine.tensor_tensor(out=norms[:, two, 0:M1], in0=part1[:, two, :], in1=sq1[:, :, :, 2], op=ALU.add)
+            engine.tensor_tensor(out=part2[:, two, :, 0], in0=part2[:, two, :, 0], in1=part2[:, two, :, 1], op=ALU.add)
+            engine.tensor_tensor(out=norms[:, two, M1:], in0=part2[:, two, :, 0], in1=sq2[:, :, :, 4], op=ALU.add)
+
+        mean_var = keep.tile([P, 2, TILES, 2], F32, name="mean_var")
         half_tiles = TILES // 2
         for lo in (0, half_tiles):
             for i in range(lo, lo + half_tiles):
@@ -111,36 +124,10 @@ def tile_interactionblock_kernel(
                     out=squares[:, i, E2 - E1 :], in_=x_e[:, i, E2:ED], func=ACT.Square,
                     scale=D2**-0.25, accum_out=square_sum[:, 1, i : i + 1],
                 )
-            four = slice(lo, lo + half_tiles)
-            sq1 = squares[:, four, 0 : E2 - E1].rearrange("p i (c d) -> p i c d", d=D1)
-            sq2 = squares[:, four, E2 - E1 :].rearrange("p i (c d) -> p i c d", d=D2)
-            nc.gpsimd.tensor_tensor(out=part1[:, four, :], in0=sq1[:, :, :, 0], in1=sq1[:, :, :, 1], op=ALU.add)
-            nc.gpsimd.tensor_tensor(out=part2[:, four, :, :], in0=sq2[:, :, :, 0:2], in1=sq2[:, :, :, 2:4], op=ALU.add)
-            nc.gpsimd.tensor_tensor(out=norms[:, four, 0:M1], in0=part1[:, four, :], in1=sq1[:, :, :, 2], op=ALU.add)
-            nc.gpsimd.tensor_tensor(
-                out=part2[:, four, :, 0], in0=part2[:, four, :, 0], in1=part2[:, four, :, 1], op=ALU.add
-            )
-            nc.gpsimd.tensor_tensor(out=norms[:, four, M1:], in0=part2[:, four, :, 0], in1=sq2[:, :, :, 4], op=ALU.add)
-        w1_words, w1_plane = weights[0]
-        w1p_words = keep.tile([P, C], U32, name="w1p_words", align_bytes=64)
-        w1p_plane = keep.tile([P, C], U8, name="w1p_plane", align_bytes=64)
-        nc.vector.tensor_copy(
-            out=w1p_words[:].bitcast(I32).rearrange("p (t m) -> p t m", t=4),
-            in_=w1_words[:].bitcast(I32).rearrange("p (m t) -> p t m", t=4),
-        )
-        nc.vector.tensor_copy(
-            out=w1p_plane[:].rearrange("p (t m) -> p m t", t=4),
-            in_=w1_plane[:].rearrange("p (m t) -> p m t", t=4),
-        )
+            component_sums(nc.gpsimd, lo, lo + half_tiles)
         for i in range(TILES):
             nc.vector.bn_aggr(out=mean_var[:, 0, i, :], in_=bn[:, 0, i, :])
             nc.vector.bn_aggr(out=mean_var[:, 1, i, :], in_=bn[:, 1, i, :])
-        centred = keep.tile([P, TILES, S], F32, name="centred")
-        for i in range(TILES):
-            nc.vector.scalar_tensor_tensor(
-                out=centred[:, i, :], in0=x_s[:, i, :], scalar=mean_var[:, 0, i, 0:1], in1=lnw_bc[:, 0:S],
-                op0=ALU.subtract, op1=ALU.mult,
-            )
         std = keep.tile([P, 4, TILES], F32, name="std")
         nc.scalar.activation(
             out=std[:, 2, :], in_=square_sum[:, 0, :], func=ACT.Sqrt, scale=math.sqrt(D1) / M1, bias=eps_col[:]
@@ -151,20 +138,39 @@ def tile_interactionblock_kernel(
         nc.scalar.activation(out=std[:, 0:2, :], in_=mean_var[:, :, :, 1], func=ACT.Sqrt, bias=eps_col[:])
         nc.scalar.activation(out=warm[:], in_=one_col[:], func=ACT.Silu)
         rstd = keep.tile([P, 4, TILES], F32, name="rstd")
-        nc.vector.reciprocal(out=rstd[:], in_=std[:])
         shift0 = keep.tile([P, TILES], F32, name="shift0")
-        nc.vector.scalar_tensor_tensor(
-            out=shift0[:], in0=mean_var[:, 1, :, 0], scalar=-1.0, in1=rstd[:, 1, :], op0=ALU.mult, op1=ALU.mult
-        )
         rvar = keep.tile([P, 2, TILES], F32, name="rvar")
-        nc.vector.tensor_tensor(out=rvar[:], in0=rstd[:, 2:4, :], in1=rstd[:, 2:4, :], op=ALU.mult)
+
+        def after_std():
+            nc.vector.reciprocal(out=rstd[:], in_=std[:])
+            nc.vector.scalar_tensor_tensor(
+                out=shift0[:], in0=mean_var[:, 1, :, 0], scalar=-1.0, in1=rstd[:, 1, :], op0=ALU.mult, op1=ALU.mult
+            )
+            nc.vector.tensor_tensor(out=rvar[:], in0=rstd[:, 2:4, :], in1=rstd[:, 2:4, :], op=ALU.mult)
 
         b2_bc = keep.tile([P, C], F32, name="b2_bc")
         nc.scalar.copy(out=b2_bc[:], in_=b2_ps[:])
         addend = keep.tile([P, TILES, C], F32, name="addend")
+
         for i in range(TILES):
             nc.gpsimd.tensor_tensor(out=addend[:, i, 0:S], in0=x_s[:, i, :], in1=b2_bc[:, 0:S], op=ALU.add)
 
+        w1_words, w1_plane = weights[0]
+        w2_words, w2_plane = weights[1]
+        w1p_words = keep.tile([P, C], U32, name="w1p_words", align_bytes=64)
+        w1p_plane = keep.tile([P, C], U8, name="w1p_plane", align_bytes=64)
+
+        def permute_w1():
+            nc.vector.tensor_copy(
+                out=w1p_words[:].bitcast(I32).rearrange("p (t m) -> p t m", t=4),
+                in_=w1_words[:].bitcast(I32).rearrange("p (m t) -> p t m", t=4),
+            )
+            nc.vector.tensor_copy(
+                out=w1p_plane[:].rearrange("p (t m) -> p m t", t=4),
+                in_=w1_plane[:].rearrange("p (m t) -> p m t", t=4),
+            )
+
+        centred = keep.tile([P, TILES, S], F32, name="centred")
         cat = keep.tile([P, TILES, C], BF16, name="cat", align_bytes=64)
         codes = keep.tile([P, 2, PAIRS, 2 * P], U32, name="codes", align_bytes=64)
         planes = keep.tile([P, 2, PAIRS, 2 * P], U8, name="planes", align_bytes=64)
@@ -177,24 +183,50 @@ def tile_interactionblock_kernel(
         h_of = {}
         hidden_of = {}
 
-        def both(pair):
-            return (2 * pair, 2 * pair + 1)
+        def invariants(pair):
+            for i in both(pair):
+                nc.scalar.activation(
+                    out=cat[:, i, S : S + M0], in_=x_e[:, i, 0:M0], func=ACT.Square,
+                    scale=rstd[:, 1, i : i + 1], bias=shift0[:, i : i + 1],
+                )
+                nc.scalar.activation(
+                    out=cat[:, i, S + M0 : S + M0 + M1], in_=norms[:, i, 0:M1], func=ACT.Copy,
+                    scale=rvar[:, 0, i : i + 1],
+                )
+                nc.scalar.activation(
+                    out=cat[:, i, S + M0 + M1 :], in_=norms[:, i, M1:], func=ACT.Copy,
+                    scale=rvar[:, 1, i : i + 1],
+                )
 
-        def turn(src, layer, pair):
+        def centre(pair):
+            for i in both(pair):
+                nc.vector.scalar_tensor_tensor(
+                    out=centred[:, i, :], in0=x_s[:, i, :], scalar=mean_var[:, 0, i, 0:1], in1=lnw_bc[:, 0:S],
+                    op0=ALU.subtract, op1=ALU.mult,
+                )
+
+        def layer_norm(pair):
+            for i in both(pair):
+                nc.vector.scalar_tensor_tensor(
+                    out=cat[:, i, 0:S], in0=centred[:, i, :], scalar=rstd[:, 0, i : i + 1], in1=lnb_bc[:, 0:S],
+                    op0=ALU.mult, op1=ALU.add,
+                )
+
+        def turn(pair):
             turned = psum_t.tile([P, 2, 2 * P], F32, name="turned")
             for half, i in enumerate(both(pair)):
-                words = src[:, i, :].bitcast(F32)
+                words = cat[:, i, :].bitcast(F32)
                 for u in range(2):
                     nc.tensor.transpose(turned[:, u, half * P : (half + 1) * P], words[:, u : C // 2 : 2], ident[:])
-            turned_of[(layer, pair)] = turned
+            turned_of[pair] = turned
 
-        def copy_out(layer, pair):
+        def copy_out_cat(pair):
             grouped = work.tile([P, 2 * P, 4], BF16, name="grouped", align_bytes=64)
             nc.scalar.copy(
                 out=grouped[:].rearrange("p r t -> p (r t)").bitcast(F32).rearrange("p (r u) -> p r u", u=2),
-                in_=turned_of[(layer, pair)][:].rearrange("p u r -> p r u"),
+                in_=turned_of[pair][:].rearrange("p u r -> p r u"),
             )
-            grouped_of[(layer, pair)] = grouped
+            grouped_of[(0, pair)] = grouped
 
         def quantise(layer, pair):
             nc.vector.quantize_mx(
@@ -220,48 +252,6 @@ def tile_interactionblock_kernel(
                     )
                 hid_of[(pair, u)] = hid
 
-        def quantise_and_multiply(layer, pair):
-            quantise(layer, pair)
-            w_words, w_plane = weights[layer]
-            for half, i in enumerate(both(pair)):
-                acc = psum_mm.tile([P, C], F32, name="acc")
-                nc.tensor.matmul_mx(
-                    out=acc[:],
-                    lhsT=codes[:, layer, pair, half * P : (half + 1) * P].bitcast(FP8X4),
-                    lhsT_scale=planes[:, layer, pair, half * P : (half + 1) * P],
-                    rhs=w_words[:].bitcast(FP8X4),
-                    rhs_scale=w_plane[:],
-                    start=True,
-                    stop=True,
-                )
-                acc_of[(layer, i)] = acc
-
-        def invariants(pair):
-            for i in both(pair):
-                nc.scalar.activation(
-                    out=cat[:, i, S : S + M0], in_=x_e[:, i, 0:M0], func=ACT.Square,
-                    scale=rstd[:, 1, i : i + 1], bias=shift0[:, i : i + 1],
-                )
-                nc.scalar.activation(
-                    out=cat[:, i, S + M0 : S + M0 + M1], in_=norms[:, i, 0:M1], func=ACT.Copy,
-                    scale=rvar[:, 0, i : i + 1],
-                )
-                nc.scalar.activation(
-                    out=cat[:, i, S + M0 + M1 :], in_=norms[:, i, M1:], func=ACT.Copy,
-                    scale=rvar[:, 1, i : i + 1],
-                )
-
-        def layer_norm(pair):
-            for i in both(pair):
-                nc.vector.scalar_tensor_tensor(
-                    out=cat[:, i, 0:S], in0=centred[:, i, :], scalar=rstd[:, 0, i : i + 1], in1=lnb_bc[:, 0:S],
-                    op0=ALU.mult, op1=ALU.add,
-                )
-            turn(cat, 0, pair)
-
-        def copy_out_cat(pair):
-            copy_out(0, pair)
-
         def activate(pair):
             hidden = work.tile([P, 4, 2 * P], BF16, name="hidden")
             for t in range(4):
@@ -271,13 +261,27 @@ def tile_interactionblock_kernel(
                 )
             hidden_of[pair] = hidden
 
-        def copy_out_hidden(pair):
+        def interleave(pair):
             grouped = work.tile([P, 2 * P, 4], BF16, name="grouped", align_bytes=64)
-            nc.vector.tensor_copy(out=grouped[:], in_=hidden_of[pair][:].rearrange("p t r -> p r t"))
+            nc.scalar.copy(out=grouped[:], in_=hidden_of[pair][:].rearrange("p t r -> p r t"))
             grouped_of[(1, pair)] = grouped
 
         def second_layer(pair):
-            quantise_and_multiply(1, pair)
+            quantise(1, pair)
+            for half, i in enumerate(both(pair)):
+                acc = psum_mm.tile([P, C], F32, name="acc")
+                nc.tensor.matmul_mx(
+                    out=acc[:],
+                    lhsT=codes[:, 1, pair, half * P : (half + 1) * P].bitcast(FP8X4),
+                    lhsT_scale=planes[:, 1, pair, half * P : (half + 1) * P],
+                    rhs=w2_words[:].bitcast(FP8X4),
+                    rhs_scale=w2_plane[:],
+                    start=True,
+                    stop=True,
+                )
+                acc_of[i] = acc
+
+        def gate_addend(pair):
             for i in both(pair):
                 for lo, hi, kind in blocks:
                     nc.scalar.activation(
@@ -285,21 +289,28 @@ def tile_interactionblock_kernel(
                         bias=std[:, kind, i : i + 1],
                     )
 
-        def gate_and_add(pair):
+        def add_up(pair):
             for i in both(pair):
                 h = keep.tile([P, C], F32, name="h%d" % i)
-                nc.vector.tensor_tensor(out=h[:], in0=acc_of[(1, i)][:], in1=addend[:, i, :], op=ALU.add)
+                nc.vector.tensor_tensor(out=h[:], in0=acc_of[i][:], in1=addend[:, i, :], op=ALU.add)
                 nc.sync.dma_start(out=out_dram[:, i, 0:S], in_=h[:, 0:S])
                 h_of[i] = h
+
+        def gate_degree0(pair):
             for i in both(pair):
                 nc.vector.scalar_tensor_tensor(
                     out=res_e[:, i, 0:M0], in0=x_e[:, i, 0:M0], scalar=mean_var[:, 1, i, 0:1],
                     in1=h_of[i][:, S : S + M0], op0=ALU.subtract, op1=ALU.mult,
                 )
+
+        def restore_mean(pair):
+            for i in both(pair):
                 nc.scalar.activation(
                     out=res_e[:, i, 0:M0], in_=res_e[:, i, 0:M0], func=ACT.Identity,
                     scale=rstd[:, 1, i : i + 1], bias=mean_var[:, 1, i, 0:1],
                 )
+
+        def gate_degree12(pair):
             for i in both(pair):
                 nc.vector.scalar_tensor_tensor(
                     out=res_e[:, i, E1:E2].rearrange("p (c d) -> p c d", d=D1),
@@ -315,12 +326,51 @@ def tile_interactionblock_kernel(
                     in1=x_e[:, i, E2:ED].rearrange("p (c d) -> p c d", d=D2),
                     op0=ALU.mult, op1=ALU.mult,
                 )
+
+        def store_equi(pair):
+            for i in both(pair):
                 nc.sync.dma_start(out=out_dram[:, i, S:], in_=res_e[:, i, :])
 
-        stages = (
-            invariants, layer_norm, copy_out_cat, first_layer, activate, copy_out_hidden, second_layer, gate_and_add
-        )
-        for step in range(PAIRS + len(stages) - 1):
-            for lag, stage in enumerate(stages):
-                if 0 <= step - lag < PAIRS:
-                    stage(step - lag)
+        centre(0)
+        after_std()
+        invariants(0)
+        layer_norm(0)
+        turn(0)
+        invariants(1)
+        centre(1)
+        layer_norm(1)
+        turn(1)
+        permute_w1()
+        copy_out_cat(0)
+        first_layer(0)
+        gate_addend(0)
+        centre(2)
+        layer_norm(2)
+        copy_out_cat(1)
+        first_layer(1)
+        gate_addend(1)
+        centre(3)
+        layer_norm(3)
+        activate(0)
+        invariants(2)
+        turn(2)
+        invariants(3)
+        turn(3)
+        for pair in range(PAIRS + 1):
+            if pair < PAIRS:
+                interleave(pair)
+            if pair >= 1:
+                add_up(pair - 1)
+            if pair < PAIRS:
+                second_layer(pair)
+            if pair + 2 < PAIRS:
+                copy_out_cat(pair + 2)
+                first_layer(pair + 2)
+                gate_addend(pair + 2)
+            if pair + 1 < PAIRS:
+                activate(pair + 1)
+            if pair >= 1:
+                gate_degree0(pair - 1)
+                restore_mean(pair - 1)
+                gate_degree12(pair - 1)
+                store_equi(pair - 1)

@@ -150,10 +150,10 @@ def tile_interactionblock_kernel(
 
         b2_bc = keep.tile([P, C], F32, name="b2_bc")
         nc.scalar.copy(out=b2_bc[:], in_=b2_ps[:])
-        addend = keep.tile([P, TILES, C], F32, name="addend")
+        addend = keep.tile([P, TILES, S], F32, name="addend")
 
         for i in range(TILES):
-            nc.gpsimd.tensor_tensor(out=addend[:, i, 0:S], in0=x_s[:, i, :], in1=b2_bc[:, 0:S], op=ALU.add)
+            nc.gpsimd.tensor_tensor(out=addend[:, i, :], in0=x_s[:, i, :], in1=b2_bc[:, 0:S], op=ALU.add)
 
         w1_words, w1_plane = weights[0]
         w2_words, w2_plane = weights[1]
@@ -281,18 +281,15 @@ def tile_interactionblock_kernel(
                 )
                 acc_of[i] = acc
 
-        def gate_addend(pair):
-            for i in both(pair):
-                for lo, hi, kind in blocks:
-                    nc.scalar.activation(
-                        out=addend[:, i, S + lo : S + hi], in_=b2_bc[:, S + lo : S + hi], func=ACT.Identity,
-                        bias=std[:, kind, i : i + 1],
-                    )
-
         def add_up(pair):
             for i in both(pair):
                 h = keep.tile([P, C], F32, name="h%d" % i)
-                nc.vector.tensor_tensor(out=h[:], in0=acc_of[i][:], in1=addend[:, i, :], op=ALU.add)
+                nc.vector.tensor_tensor(out=h[:, 0:S], in0=acc_of[i][:, 0:S], in1=addend[:, i, :], op=ALU.add)
+                for lo, hi, kind in blocks:
+                    nc.vector.scalar_tensor_tensor(
+                        out=h[:, S + lo : S + hi], in0=acc_of[i][:, S + lo : S + hi], scalar=std[:, kind, i : i + 1],
+                        in1=b2_bc[:, S + lo : S + hi], op0=ALU.add, op1=ALU.add,
+                    )
                 nc.sync.dma_start(out=out_dram[:, i, 0:S], in_=h[:, 0:S])
                 h_of[i] = h
 
@@ -305,9 +302,9 @@ def tile_interactionblock_kernel(
 
         def restore_mean(pair):
             for i in both(pair):
-                nc.scalar.activation(
-                    out=res_e[:, i, 0:M0], in_=res_e[:, i, 0:M0], func=ACT.Identity,
-                    scale=rstd[:, 1, i : i + 1], bias=mean_var[:, 1, i, 0:1],
+                nc.vector.tensor_scalar(
+                    out=res_e[:, i, 0:M0], in0=res_e[:, i, 0:M0], scalar1=rstd[:, 1, i : i + 1],
+                    scalar2=mean_var[:, 1, i, 0:1], op0=ALU.mult, op1=ALU.add,
                 )
 
         def gate_degree12(pair):
@@ -343,12 +340,10 @@ def tile_interactionblock_kernel(
         permute_w1()
         copy_out_cat(0)
         first_layer(0)
-        gate_addend(0)
         centre(2)
         layer_norm(2)
         copy_out_cat(1)
         first_layer(1)
-        gate_addend(1)
         centre(3)
         layer_norm(3)
         activate(0)
@@ -366,11 +361,10 @@ def tile_interactionblock_kernel(
             if pair + 2 < PAIRS:
                 copy_out_cat(pair + 2)
                 first_layer(pair + 2)
-                gate_addend(pair + 2)
             if pair + 1 < PAIRS:
                 activate(pair + 1)
             if pair >= 1:
                 gate_degree0(pair - 1)
-                restore_mean(pair - 1)
                 gate_degree12(pair - 1)
+                restore_mean(pair - 1)
                 store_equi(pair - 1)

@@ -293,21 +293,12 @@ def tile_interactionblock_kernel(
                 nc.sync.dma_start(out=out_dram[:, i, 0:S], in_=h[:, 0:S])
                 h_of[i] = h
 
-        def gate_degree0(pair):
+        def gate(pair):
             for i in both(pair):
                 nc.vector.scalar_tensor_tensor(
                     out=res_e[:, i, 0:M0], in0=x_e[:, i, 0:M0], scalar=mean_var[:, 1, i, 0:1],
                     in1=h_of[i][:, S : S + M0], op0=ALU.subtract, op1=ALU.mult,
                 )
-
-        def restore_mean(pair):
-            for i in both(pair):
-                nc.vector.tensor_scalar(
-                    out=res_e[:, i, 0:M0], in0=res_e[:, i, 0:M0], scalar1=rstd[:, 1, i : i + 1],
-                    scalar2=mean_var[:, 1, i, 0:1], op0=ALU.mult, op1=ALU.add,
-                )
-
-        def gate_degree12(pair):
             for i in both(pair):
                 nc.vector.scalar_tensor_tensor(
                     out=res_e[:, i, E1:E2].rearrange("p (c d) -> p c d", d=D1),
@@ -316,6 +307,10 @@ def tile_interactionblock_kernel(
                     in1=x_e[:, i, E1:E2].rearrange("p (c d) -> p c d", d=D1),
                     op0=ALU.mult, op1=ALU.mult,
                 )
+                nc.vector.tensor_scalar(
+                    out=res_e[:, i, 0:M0], in0=res_e[:, i, 0:M0], scalar1=rstd[:, 1, i : i + 1],
+                    scalar2=mean_var[:, 1, i, 0:1], op0=ALU.mult, op1=ALU.add,
+                )
                 nc.vector.scalar_tensor_tensor(
                     out=res_e[:, i, E2:ED].rearrange("p (c d) -> p c d", d=D2),
                     in0=h_of[i][:, S + M0 + M1 :].unsqueeze(2).to_broadcast([P, M2, D2]),
@@ -323,9 +318,6 @@ def tile_interactionblock_kernel(
                     in1=x_e[:, i, E2:ED].rearrange("p (c d) -> p c d", d=D2),
                     op0=ALU.mult, op1=ALU.mult,
                 )
-
-        def store_equi(pair):
-            for i in both(pair):
                 nc.sync.dma_start(out=out_dram[:, i, S:], in_=res_e[:, i, :])
 
         centre(0)
@@ -364,7 +356,4 @@ def tile_interactionblock_kernel(
             if pair + 1 < PAIRS:
                 activate(pair + 1)
             if pair >= 1:
-                gate_degree0(pair - 1)
-                gate_degree12(pair - 1)
-                restore_mean(pair - 1)
-                store_equi(pair - 1)
+                gate(pair - 1)

@@ -56,7 +56,7 @@ def tile_interactionblock_kernel(
             nc.sync.dma_start(out=x_s[:, two, :], in_=xs_dram[:, two, :])
             nc.sync.dma_start(out=x_e[:, two, :], in_=xe_dram[:, two, :])
 
-        vec_rows = keep.tile([P, 3, C], BF16, name="vec_rows")
+        vec_rows = keep.tile([P, 2, C], BF16, name="vec_rows")
         nc.vector.memset(vec_rows[:].rearrange("p v c -> p (v c)").bitcast(I32), 0)
         one_col = keep.tile([P, 1], F32, name="one_col")
         nc.vector.memset(one_col[:], 1.0)
@@ -66,11 +66,11 @@ def tile_interactionblock_kernel(
         nc.vector.memset(eps_col[:], EPS)
         warm = keep.tile([P, 1], F32, name="warm")
         nc.scalar.activation(out=warm[:], in_=one_col[:], func=ACT.Sqrt)
-        vectors = (ln_w, ln_b, b2)
+        vectors = (ln_w, ln_b)
         for v, vec in enumerate(vectors):
-            nc.scalar.dma_start(out=vec_rows[0:1, v, 0 : vec.shape[0]], in_=vec.rearrange("(o c) -> o c", o=1))
+            nc.sync.dma_start(out=vec_rows[0:1, v, 0 : vec.shape[0]], in_=vec.rearrange("(o c) -> o c", o=1))
         b1_col = keep.tile([P, 4], BF16, name="b1_col")
-        nc.scalar.dma_start(out=b1_col[:], in_=b1.rearrange("(p t) -> p t", t=4))
+        nc.sync.dma_start(out=b1_col[:], in_=b1.rearrange("(p t) -> p t", t=4))
         ident = keep.tile([P, P], F32, name="ident")
         make_identity(nc, ident[:])
 
@@ -87,10 +87,12 @@ def tile_interactionblock_kernel(
                 )
             weights.append((words, plane))
 
+        b2_bc = keep.tile([P, C], BF16, name="b2_bc")
+        nc.sync.dma_start(out=b2_bc[:], in_=b2.partition_broadcast(P))
+
         lnw_bc = psum_ln.tile([P, C], F32, name="lnw_bc")
         lnb_bc = psum_ln.tile([P, C], F32, name="lnb_bc")
-        b2_ps = psum_mm.tile([P, C], F32, name="b2_ps", tag="acc")
-        for v, spread in enumerate((lnw_bc, lnb_bc, b2_ps)):
+        for v, spread in enumerate((lnw_bc, lnb_bc)):
             nc.tensor.matmul(out=spread[:], lhsT=ones_sq[:], rhs=vec_rows[:, v, :], start=True, stop=True)
 
         bn = keep.tile([P, 2, TILES, 6], F32, name="bn")
@@ -148,8 +150,6 @@ def tile_interactionblock_kernel(
             )
             nc.vector.tensor_tensor(out=rvar[:], in0=rstd[:, 2:4, :], in1=rstd[:, 2:4, :], op=ALU.mult)
 
-        b2_bc = keep.tile([P, C], F32, name="b2_bc")
-        nc.scalar.copy(out=b2_bc[:], in_=b2_ps[:])
         addend = keep.tile([P, TILES, S], F32, name="addend")
 
         for i in range(TILES):
@@ -174,7 +174,8 @@ def tile_interactionblock_kernel(
         cat = keep.tile([P, TILES, C], BF16, name="cat", align_bytes=64)
         codes = keep.tile([P, 2, PAIRS, 2 * P], U32, name="codes", align_bytes=64)
         planes = keep.tile([P, 2, PAIRS, 2 * P], U8, name="planes", align_bytes=64)
-        res_e = keep.tile([P, TILES, ED], F32, name="res_e")
+        res_e = keep.tile([P, TILES, E2], F32, name="res_e")
+        res_2 = keep.tile([P, TILES, ED - E2], F32, name="res_2")
         blocks = ((0, M0, 1), (M0, M0 + M1, 2), (M0 + M1, NI, 3))
         turned_of = {}
         grouped_of = {}
@@ -311,14 +312,15 @@ def tile_interactionblock_kernel(
                     out=res_e[:, i, 0:M0], in0=res_e[:, i, 0:M0], scalar1=rstd[:, 1, i : i + 1],
                     scalar2=mean_var[:, 1, i, 0:1], op0=ALU.mult, op1=ALU.add,
                 )
+                nc.sync.dma_start(out=out_dram[:, i, S : S + E2], in_=res_e[:, i, :])
                 nc.vector.scalar_tensor_tensor(
-                    out=res_e[:, i, E2:ED].rearrange("p (c d) -> p c d", d=D2),
+                    out=res_2[:, i, :].rearrange("p (c d) -> p c d", d=D2),
                     in0=h_of[i][:, S + M0 + M1 :].unsqueeze(2).to_broadcast([P, M2, D2]),
                     scalar=rstd[:, 3, i : i + 1],
                     in1=x_e[:, i, E2:ED].rearrange("p (c d) -> p c d", d=D2),
                     op0=ALU.mult, op1=ALU.mult,
                 )
-                nc.sync.dma_start(out=out_dram[:, i, S:], in_=res_e[:, i, :])
+                nc.sync.dma_start(out=out_dram[:, i, S + E2 :], in_=res_2[:, i, :])
 
         centre(0)
         after_std()

@@ -152,8 +152,11 @@ def tile_interactionblock_kernel(
 
         addend = keep.tile([P, TILES, S], F32, name="addend")
 
-        for i in range(TILES):
-            nc.gpsimd.tensor_tensor(out=addend[:, i, :], in0=x_s[:, i, :], in1=b2_bc[:, 0:S], op=ALU.add)
+        for pair in range(PAIRS):
+            two = slice(2 * pair, 2 * pair + 2)
+            nc.gpsimd.tensor_tensor(
+                out=addend[:, two, :], in0=x_s[:, two, :], in1=b2_bc[:, 0:S].unsqueeze(1).to_broadcast([P, 2, S]), op=ALU.add
+            )
 
         w1_words, w1_plane = weights[0]
         w2_words, w2_plane = weights[1]
@@ -308,10 +311,16 @@ def tile_interactionblock_kernel(
                     in1=x_e[:, i, E1:E2].rearrange("p (c d) -> p c d", d=D1),
                     op0=ALU.mult, op1=ALU.mult,
                 )
-                nc.vector.tensor_scalar(
-                    out=res_e[:, i, 0:M0], in0=res_e[:, i, 0:M0], scalar1=rstd[:, 1, i : i + 1],
-                    scalar2=mean_var[:, 1, i, 0:1], op0=ALU.mult, op1=ALU.add,
-                )
+                if pair < PAIRS - 1:
+                    nc.scalar.activation(
+                        out=res_e[:, i, 0:M0], in_=res_e[:, i, 0:M0], func=ACT.Identity,
+                        scale=rstd[:, 1, i : i + 1], bias=mean_var[:, 1, i, 0:1],
+                    )
+                else:
+                    nc.vector.tensor_scalar(
+                        out=res_e[:, i, 0:M0], in0=res_e[:, i, 0:M0], scalar1=rstd[:, 1, i : i + 1],
+                        scalar2=mean_var[:, 1, i, 0:1], op0=ALU.mult, op1=ALU.add,
+                    )
                 nc.sync.dma_start(out=out_dram[:, i, S : S + E2], in_=res_e[:, i, :])
                 nc.vector.scalar_tensor_tensor(
                     out=res_2[:, i, :].rearrange("p (c d) -> p c d", d=D2),

@@ -311,16 +311,10 @@ def tile_interactionblock_kernel(
                     in1=x_e[:, i, E1:E2].rearrange("p (c d) -> p c d", d=D1),
                     op0=ALU.mult, op1=ALU.mult,
                 )
-                if pair < PAIRS - 1:
-                    nc.scalar.activation(
-                        out=res_e[:, i, 0:M0], in_=res_e[:, i, 0:M0], func=ACT.Identity,
-                        scale=rstd[:, 1, i : i + 1], bias=mean_var[:, 1, i, 0:1],
-                    )
-                else:
-                    nc.vector.tensor_scalar(
-                        out=res_e[:, i, 0:M0], in0=res_e[:, i, 0:M0], scalar1=rstd[:, 1, i : i + 1],
-                        scalar2=mean_var[:, 1, i, 0:1], op0=ALU.mult, op1=ALU.add,
-                    )
+                nc.scalar.activation(
+                    out=res_e[:, i, 0:M0], in_=res_e[:, i, 0:M0], func=ACT.Identity,
+                    scale=rstd[:, 1, i : i + 1], bias=mean_var[:, 1, i, 0:1],
+                )
                 nc.sync.dma_start(out=out_dram[:, i, S : S + E2], in_=res_e[:, i, :])
                 nc.vector.scalar_tensor_tensor(
                     out=res_2[:, i, :].rearrange("p (c d) -> p c d", d=D2),

@@ -26,6 +26,7 @@ ED = E2 + M2 * D2
 NI = M0 + M1 + M2
 C = S + NI
 EPS = 1e-5
+BN_COLUMNS = 256
 
 FLOPS = 2 * 2 * ROWS * C * C
 
@@ -95,7 +96,8 @@ def tile_interactionblock_kernel(
         for v, spread in enumerate((lnw_bc, lnb_bc)):
             nc.tensor.matmul(out=spread[:], lhsT=ones_sq[:], rhs=vec_rows[:, v, :], start=True, stop=True)
 
-        bn = keep.tile([P, 2, TILES, 6], F32, name="bn")
+        bn_s = keep.tile([P, PAIRS, 2, 2, 3], F32, name="bn_s")
+        bn_e = keep.tile([P, TILES, 3], F32, name="bn_e")
         squares = keep.tile([P, TILES, ED - E1], F32, name="squares")
         square_sum = keep.tile([P, 2, TILES], F32, name="square_sum")
         norms = keep.tile([P, TILES, M1 + M2], F32, name="norms")
@@ -112,12 +114,20 @@ def tile_interactionblock_kernel(
             engine.tensor_tensor(out=part2[:, two, :, 0], in0=part2[:, two, :, 0], in1=part2[:, two, :, 1], op=ALU.add)
             engine.tensor_tensor(out=norms[:, two, M1:], in0=part2[:, two, :, 0], in1=sq2[:, :, :, 4], op=ALU.add)
 
-        mean_var = keep.tile([P, 2, TILES, 2], F32, name="mean_var")
+        mean_var = keep.tile([P, TILES, 2], F32, name="mean_var")
         half_tiles = TILES // 2
         for lo in (0, half_tiles):
             for i in range(lo, lo + half_tiles):
-                nc.vector.bn_stats(out=bn[:, 0, i, :], in_=x_s[:, i, :])
-                nc.vector.bn_stats(out=bn[:, 1, i, :], in_=x_e[:, i, 0:M0])
+                if i % 2 == 0:
+                    two = slice(i, i + 2)
+                    for part, columns in enumerate((slice(0, BN_COLUMNS), slice(BN_COLUMNS, S))):
+                        nc.vector.bn_stats(
+                            out=bn_s[:, i // 2, part, :, :].rearrange("p i f -> p (i f)"),
+                            in_=x_s[:, two, columns].rearrange("p i s -> p s i"),
+                        )
+                    nc.vector.bn_stats(
+                        out=bn_e[:, two, :].rearrange("p i f -> p (i f)"), in_=x_e[:, two, 0:M0].rearrange("p i s -> p s i")
+                    )
                 nc.scalar.activation(
                     out=squares[:, i, 0 : E2 - E1], in_=x_e[:, i, E1:E2], func=ACT.Square,
                     scale=D1**-0.25, accum_out=square_sum[:, 0, i : i + 1],
@@ -128,8 +138,7 @@ def tile_interactionblock_kernel(
                 )
             component_sums(nc.gpsimd, lo, lo + half_tiles)
         for i in range(TILES):
-            nc.vector.bn_aggr(out=mean_var[:, 0, i, :], in_=bn[:, 0, i, :])
-            nc.vector.bn_aggr(out=mean_var[:, 1, i, :], in_=bn[:, 1, i, :])
+            nc.vector.bn_aggr(out=mean_var[:, i, :], in_=bn_s[:, i // 2, :, i % 2, :])
         std = keep.tile([P, 4, TILES], F32, name="std")
         nc.scalar.activation(
             out=std[:, 2, :], in_=square_sum[:, 0, :], func=ACT.Sqrt, scale=math.sqrt(D1) / M1, bias=eps_col[:]
@@ -137,7 +146,8 @@ def tile_interactionblock_kernel(
         nc.scalar.activation(
             out=std[:, 3, :], in_=square_sum[:, 1, :], func=ACT.Sqrt, scale=math.sqrt(D2) / M2, bias=eps_col[:]
         )
-        nc.scalar.activation(out=std[:, 0:2, :], in_=mean_var[:, :, :, 1], func=ACT.Sqrt, bias=eps_col[:])
+        nc.scalar.activation(out=std[:, 1, :], in_=bn_e[:, :, 2], func=ACT.Sqrt, scale=1.0 / M0, bias=eps_col[:])
+        nc.scalar.activation(out=std[:, 0, :], in_=mean_var[:, :, 1], func=ACT.Sqrt, bias=eps_col[:])
         nc.scalar.activation(out=warm[:], in_=one_col[:], func=ACT.Silu)
         rstd = keep.tile([P, 4, TILES], F32, name="rstd")
         shift0 = keep.tile([P, TILES], F32, name="shift0")
@@ -146,7 +156,7 @@ def tile_interactionblock_kernel(
         def after_std():
             nc.vector.reciprocal(out=rstd[:], in_=std[:])
             nc.vector.scalar_tensor_tensor(
-                out=shift0[:], in0=mean_var[:, 1, :, 0], scalar=-1.0, in1=rstd[:, 1, :], op0=ALU.mult, op1=ALU.mult
+                out=shift0[:], in0=bn_e[:, :, 1], scalar=-1.0, in1=rstd[:, 1, :], op0=ALU.mult, op1=ALU.mult
             )
             nc.vector.tensor_tensor(out=rvar[:], in0=rstd[:, 2:4, :], in1=rstd[:, 2:4, :], op=ALU.mult)
 
@@ -205,7 +215,7 @@ def tile_interactionblock_kernel(
         def centre(pair):
             for i in both(pair):
                 nc.vector.scalar_tensor_tensor(
-                    out=centred[:, i, :], in0=x_s[:, i, :], scalar=mean_var[:, 0, i, 0:1], in1=lnw_bc[:, 0:S],
+                    out=centred[:, i, :], in0=x_s[:, i, :], scalar=mean_var[:, i, 0:1], in1=lnw_bc[:, 0:S],
                     op0=ALU.subtract, op1=ALU.mult,
                 )
 
@@ -300,7 +310,7 @@ def tile_interactionblock_kernel(
         def gate(pair):
             for i in both(pair):
                 nc.vector.scalar_tensor_tensor(
-                    out=res_e[:, i, 0:M0], in0=x_e[:, i, 0:M0], scalar=mean_var[:, 1, i, 0:1],
+                    out=res_e[:, i, 0:M0], in0=x_e[:, i, 0:M0], scalar=bn_e[:, i, 1:2],
                     in1=h_of[i][:, S : S + M0], op0=ALU.subtract, op1=ALU.mult,
                 )
             for i in both(pair):
@@ -313,7 +323,7 @@ def tile_interactionblock_kernel(
                 )
                 nc.scalar.activation(
                     out=res_e[:, i, 0:M0], in_=res_e[:, i, 0:M0], func=ACT.Identity,
-                    scale=rstd[:, 1, i : i + 1], bias=mean_var[:, 1, i, 0:1],
+                    scale=rstd[:, 1, i : i + 1], bias=bn_e[:, i, 1:2],
                 )
                 nc.sync.dma_start(out=out_dram[:, i, S : S + E2], in_=res_e[:, i, :])
                 nc.vector.scalar_tensor_tensor(

@@ -187,8 +187,8 @@ def tile_interactionblock_kernel(
         cat = keep.tile([P, TILES, C], BF16, name="cat", align_bytes=64)
         codes = keep.tile([P, 2, PAIRS, 2 * P], U32, name="codes", align_bytes=64)
         planes = keep.tile([P, 2, PAIRS, 2 * P], U8, name="planes", align_bytes=64)
-        res_e = keep.tile([P, TILES, E2], F32, name="res_e")
-        res_2 = keep.tile([P, TILES, ED - E2], F32, name="res_2")
+        res_s = keep.tile([P, TILES, S], F32, name="res_s")
+        res_e = keep.tile([P, TILES, ED], F32, name="res_e")
         blocks = ((0, M0, 1), (M0, M0 + M1, 2), (M0 + M1, NI, 3))
         turned_of = {}
         grouped_of = {}
@@ -277,7 +277,8 @@ def tile_interactionblock_kernel(
 
         def interleave(pair):
             grouped = work.tile([P, 2 * P, 4], BF16, name="grouped", align_bytes=64)
-            nc.scalar.copy(out=grouped[:], in_=hidden_of[pair][:].rearrange("p t r -> p r t"))
+            copy = nc.vector.tensor_copy if pair == 0 else nc.scalar.copy
+            copy(out=grouped[:], in_=hidden_of[pair][:].rearrange("p t r -> p r t"))
             grouped_of[(1, pair)] = grouped
 
         def second_layer(pair):
@@ -297,26 +298,27 @@ def tile_interactionblock_kernel(
 
         def add_up(pair):
             for i in both(pair):
-                h = keep.tile([P, C], F32, name="h%d" % i)
-                nc.vector.tensor_tensor(out=h[:, 0:S], in0=acc_of[i][:, 0:S], in1=addend[:, i, :], op=ALU.add)
+                h = keep.tile([P, NI], F32, name="h%d" % i)
+                nc.vector.tensor_tensor(out=res_s[:, i, :], in0=acc_of[i][:, 0:S], in1=addend[:, i, :], op=ALU.add)
                 for lo, hi, kind in blocks:
                     nc.vector.scalar_tensor_tensor(
-                        out=h[:, S + lo : S + hi], in0=acc_of[i][:, S + lo : S + hi], scalar=std[:, kind, i : i + 1],
+                        out=h[:, lo:hi], in0=acc_of[i][:, S + lo : S + hi], scalar=std[:, kind, i : i + 1],
                         in1=b2_bc[:, S + lo : S + hi], op0=ALU.add, op1=ALU.add,
                     )
-                nc.sync.dma_start(out=out_dram[:, i, 0:S], in_=h[:, 0:S])
                 h_of[i] = h
+            two = slice(2 * pair, 2 * pair + 2)
+            nc.sync.dma_start(out=out_dram[:, two, 0:S], in_=res_s[:, two, :])
 
         def gate(pair):
             for i in both(pair):
                 nc.vector.scalar_tensor_tensor(
                     out=res_e[:, i, 0:M0], in0=x_e[:, i, 0:M0], scalar=bn_e[:, i, 1:2],
-                    in1=h_of[i][:, S : S + M0], op0=ALU.subtract, op1=ALU.mult,
+                    in1=h_of[i][:, 0:M0], op0=ALU.subtract, op1=ALU.mult,
                 )
             for i in both(pair):
                 nc.vector.scalar_tensor_tensor(
                     out=res_e[:, i, E1:E2].rearrange("p (c d) -> p c d", d=D1),
-                    in0=h_of[i][:, S + M0 : S + M0 + M1].unsqueeze(2).to_broadcast([P, M1, D1]),
+                    in0=h_of[i][:, M0 : M0 + M1].unsqueeze(2).to_broadcast([P, M1, D1]),
                     scalar=rstd[:, 2, i : i + 1],
                     in1=x_e[:, i, E1:E2].rearrange("p (c d) -> p c d", d=D1),
                     op0=ALU.mult, op1=ALU.mult,
@@ -325,15 +327,14 @@ def tile_interactionblock_kernel(
                     out=res_e[:, i, 0:M0], in_=res_e[:, i, 0:M0], func=ACT.Identity,
                     scale=rstd[:, 1, i : i + 1], bias=bn_e[:, i, 1:2],
                 )
-                nc.sync.dma_start(out=out_dram[:, i, S : S + E2], in_=res_e[:, i, :])
                 nc.vector.scalar_tensor_tensor(
-                    out=res_2[:, i, :].rearrange("p (c d) -> p c d", d=D2),
-                    in0=h_of[i][:, S + M0 + M1 :].unsqueeze(2).to_broadcast([P, M2, D2]),
+                    out=res_e[:, i, E2:].rearrange("p (c d) -> p c d", d=D2),
+                    in0=h_of[i][:, M0 + M1 :].unsqueeze(2).to_broadcast([P, M2, D2]),
                     scalar=rstd[:, 3, i : i + 1],
                     in1=x_e[:, i, E2:ED].rearrange("p (c d) -> p c d", d=D2),
                     op0=ALU.mult, op1=ALU.mult,
                 )
-                nc.sync.dma_start(out=out_dram[:, i, S + E2 :], in_=res_2[:, i, :])
+                nc.sync.dma_start(out=out_dram[:, i, S:], in_=res_e[:, i, :])
 
         centre(0)
         after_std()

@@ -160,13 +160,21 @@ def tile_interactionblock_kernel(
             )
             nc.vector.tensor_tensor(out=rvar[:], in0=rstd[:, 2:4, :], in1=rstd[:, 2:4, :], op=ALU.mult)
 
-        addend = keep.tile([P, TILES, S], F32, name="addend")
+        addend_of = {}
 
-        for pair in range(PAIRS):
-            two = slice(2 * pair, 2 * pair + 2)
-            nc.gpsimd.tensor_tensor(
-                out=addend[:, two, :], in0=x_s[:, two, :], in1=b2_bc[:, 0:S].unsqueeze(1).to_broadcast([P, 2, S]), op=ALU.add
+        def add_node_scalar(pair):
+            if pair < PAIRS - 2:
+                addend = keep.tile([P, 2, S], F32, name="addend%d" % pair, align_bytes=64)
+            else:
+                addend = keep.tile([P, 2, S], F32, name="late%d" % pair, align_bytes=64)
+            engine = nc.vector if pair == 1 else nc.gpsimd
+            engine.tensor_tensor(
+                out=addend[:], in0=x_s[:, 2 * pair : 2 * pair + 2, :],
+                in1=b2_bc[:, 0:S].unsqueeze(1).to_broadcast([P, 2, S]), op=ALU.add,
             )
+            addend_of[pair] = addend
+
+        add_node_scalar(0)
 
         w1_words, w1_plane = weights[0]
         w2_words, w2_plane = weights[1]
@@ -235,7 +243,10 @@ def tile_interactionblock_kernel(
             turned_of[pair] = turned
 
         def copy_out_cat(pair):
-            grouped = work.tile([P, 2 * P, 4], BF16, name="grouped", align_bytes=64)
+            if pair < PAIRS - 2:
+                grouped = work.tile([P, 2 * P, 4], BF16, name="grouped", align_bytes=64)
+            else:
+                grouped = keep.tile([P, 2 * P, 4], BF16, name="late%d" % pair, align_bytes=64)
             nc.scalar.copy(
                 out=grouped[:].rearrange("p r t -> p (r t)").bitcast(F32).rearrange("p (r u) -> p r u", u=2),
                 in_=turned_of[pair][:].rearrange("p u r -> p r u"),
@@ -299,7 +310,7 @@ def tile_interactionblock_kernel(
         def add_up(pair):
             for i in both(pair):
                 h = keep.tile([P, NI], F32, name="h%d" % i)
-                nc.vector.tensor_tensor(out=res_s[:, i, :], in0=acc_of[i][:, 0:S], in1=addend[:, i, :], op=ALU.add)
+                nc.vector.tensor_tensor(out=res_s[:, i, :], in0=acc_of[i][:, 0:S], in1=addend_of[pair][:, i % 2, :], op=ALU.add)
                 for lo, hi, kind in blocks:
                     nc.vector.scalar_tensor_tensor(
                         out=h[:, lo:hi], in0=acc_of[i][:, S + lo : S + hi], scalar=std[:, kind, i : i + 1],
@@ -315,7 +326,6 @@ def tile_interactionblock_kernel(
                     out=res_e[:, i, 0:M0], in0=x_e[:, i, 0:M0], scalar=bn_e[:, i, 1:2],
                     in1=h_of[i][:, 0:M0], op0=ALU.subtract, op1=ALU.mult,
                 )
-            for i in both(pair):
                 nc.vector.scalar_tensor_tensor(
                     out=res_e[:, i, E1:E2].rearrange("p (c d) -> p c d", d=D1),
                     in0=h_of[i][:, M0 : M0 + M1].unsqueeze(2).to_broadcast([P, M1, D1]),
@@ -323,16 +333,19 @@ def tile_interactionblock_kernel(
                     in1=x_e[:, i, E1:E2].rearrange("p (c d) -> p c d", d=D1),
                     op0=ALU.mult, op1=ALU.mult,
                 )
-                nc.scalar.activation(
-                    out=res_e[:, i, 0:M0], in_=res_e[:, i, 0:M0], func=ACT.Identity,
-                    scale=rstd[:, 1, i : i + 1], bias=bn_e[:, i, 1:2],
-                )
                 nc.vector.scalar_tensor_tensor(
                     out=res_e[:, i, E2:].rearrange("p (c d) -> p c d", d=D2),
                     in0=h_of[i][:, M0 + M1 :].unsqueeze(2).to_broadcast([P, M2, D2]),
                     scalar=rstd[:, 3, i : i + 1],
                     in1=x_e[:, i, E2:ED].rearrange("p (c d) -> p c d", d=D2),
                     op0=ALU.mult, op1=ALU.mult,
+                )
+
+        def mean_back(pair):
+            for i in both(pair):
+                nc.scalar.activation(
+                    out=res_e[:, i, 0:M0], in_=res_e[:, i, 0:M0], func=ACT.Identity,
+                    scale=rstd[:, 1, i : i + 1], bias=bn_e[:, i, 1:2],
                 )
                 nc.sync.dma_start(out=out_dram[:, i, S:], in_=res_e[:, i, :])
 
@@ -366,10 +379,16 @@ def tile_interactionblock_kernel(
                 add_up(pair - 1)
             if pair < PAIRS:
                 second_layer(pair)
+            if pair == 0:
+                add_node_scalar(1)
             if pair + 2 < PAIRS:
                 copy_out_cat(pair + 2)
+            if pair >= 1:
+                gate(pair - 1)
+            if pair + 2 < PAIRS:
                 first_layer(pair + 2)
+                add_node_scalar(pair + 2)
             if pair + 1 < PAIRS:
                 activate(pair + 1)
             if pair >= 1:
-                gate(pair - 1)
+                mean_back(pair - 1)

@@ -242,6 +242,10 @@ def tile_interactionblock_kernel(
                     nc.tensor.transpose(turned[:, u, half * P : (half + 1) * P], words[:, u : C // 2 : 2], ident[:])
             turned_of[pair] = turned
 
+        def keep_warm(i):
+            spare = psum_mm.tile([P, C], F32, name="acc")
+            nc.tensor.matmul(out=spare[:], lhsT=ones_sq[:], rhs=cat[:, i, :], start=True, stop=True)
+
         def copy_out_cat(pair):
             if pair < PAIRS - 2:
                 grouped = work.tile([P, 2 * P, 4], BF16, name="grouped", align_bytes=64)
@@ -354,10 +358,13 @@ def tile_interactionblock_kernel(
         invariants(0)
         layer_norm(0)
         turn(0)
+        keep_warm(0)
+        keep_warm(1)
         invariants(1)
         centre(1)
         layer_norm(1)
         turn(1)
+        keep_warm(3)
         permute_w1()
         copy_out_cat(0)
         first_layer(0)
@@ -370,6 +377,7 @@ def tile_interactionblock_kernel(
         activate(0)
         invariants(2)
         turn(2)
+        keep_warm(4)
         invariants(3)
         turn(3)
         for pair in range(PAIRS + 1):

import math
from contextlib import ExitStack

import concourse.mybir as mybir
from concourse.masks import make_identity

F32 = mybir.dt.float32
BF16 = mybir.dt.bfloat16
I32 = mybir.dt.int32
U32 = mybir.dt.uint32
U8 = mybir.dt.uint8
FP8X4 = mybir.dt.float8_e4m3fn_x4
ALU = mybir.AluOpType
ACT = mybir.ActivationFunctionType

P = 128
ROWS = 1024
TILES = ROWS // P
PAIRS = TILES // 2
S = 288
M0, M1, M2 = 128, 64, 32
D1, D2 = 3, 5
E1 = M0
E2 = M0 + M1 * D1
ED = E2 + M2 * D2
NI = M0 + M1 + M2
C = S + NI
EPS = 1e-5
BN_COLUMNS = 256

FLOPS = 2 * 2 * ROWS * C * C


def tile_interactionblock_kernel(
    tc, node_scalar, node_equi, ln_w, ln_b, W1_words, W1_scales, b1, W2_words, W2_scales, b2, out
):
    nc = tc.nc
    xs_dram = node_scalar.rearrange("(p i) s -> p i s", i=TILES)
    xe_dram = node_equi.rearrange("(p i) e -> p i e", i=TILES)
    out_dram = out.rearrange("(p i) c -> p i c", i=TILES)

    with ExitStack() as ctx:
        keep = ctx.enter_context(tc.tile_pool(name="keep", bufs=1))
        work = ctx.enter_context(tc.tile_pool(name="work", bufs=3))
        psum_ln = ctx.enter_context(tc.psum_pool(name="psum_ln", bufs=1))
        psum_t = ctx.enter_context(tc.psum_pool(name="psum_t", bufs=2))
        psum_mm = ctx.enter_context(tc.psum_pool(name="psum_mm", bufs=2))
        ctx.enter_context(tc.manual_schedule())

        def both(pair):
            return (2 * pair, 2 * pair + 1)

        x_s = keep.tile([P, TILES, S], BF16, name="x_s")
        x_e = keep.tile([P, TILES, ED], BF16, name="x_e")
        for pair in range(PAIRS):
            two = slice(2 * pair, 2 * pair + 2)
            nc.sync.dma_start(out=x_s[:, two, :], in_=xs_dram[:, two, :])
            nc.sync.dma_start(out=x_e[:, two, :], in_=xe_dram[:, two, :])

        vec_rows = keep.tile([P, 2, C], BF16, name="vec_rows")
        nc.vector.memset(vec_rows[:].rearrange("p v c -> p (v c)").bitcast(I32), 0)
        one_col = keep.tile([P, 1], F32, name="one_col")
        nc.vector.memset(one_col[:], 1.0)
        ones_sq = keep.tile([P, P], BF16, name="ones_sq")
        nc.vector.memset(ones_sq[:], 1.0)
        eps_col = keep.tile([P, 1], F32, name="eps_col")
        nc.vector.memset(eps_col[:], EPS)
        warm = keep.tile([P, 1], F32, name="warm")
        nc.scalar.activation(out=warm[:], in_=one_col[:], func=ACT.Sqrt)
        vectors = (ln_w, ln_b)
        for v, vec in enumerate(vectors):
            nc.sync.dma_start(out=vec_rows[0:1, v, 0 : vec.shape[0]], in_=vec.rearrange("(o c) -> o c", o=1))
        b1_col = keep.tile([P, 4], BF16, name="b1_col")
        nc.sync.dma_start(out=b1_col[:], in_=b1.rearrange("(p t) -> p t", t=4))
        ident = keep.tile([P, P], F32, name="ident")
        make_identity(nc, ident[:])

        weights = []
        for name, words_dram, scales_dram in (("w1", W1_words, W1_scales), ("w2", W2_words, W2_scales)):
            words = keep.tile([P, 4 * C], U8, name=name + "_words", align_bytes=64)
            plane = keep.tile([P, C], U8, name=name + "_plane", align_bytes=64)
            nc.vector.memset(plane[:].bitcast(I32), 0)
            nc.sync.dma_start(out=words[:].bitcast(I32), in_=words_dram[0].rearrange("p n t -> p (n t)").bitcast(I32))
            for quad in range(4):
                nc.sync.dma_start(
                    out=plane[32 * quad : 32 * quad + 4, :].bitcast(I32),
                    in_=scales_dram[0, 4 * quad : 4 * quad + 4, :].bitcast(I32),
                )
            weights.append((words, plane))

        b2_bc = keep.tile([P, C], BF16, name="b2_bc")
        nc.sync.dma_start(out=b2_bc[:], in_=b2.partition_broadcast(P))

        lnw_bc = psum_ln.tile([P, C], F32, name="lnw_bc")
        lnb_bc = psum_ln.tile([P, C], F32, name="lnb_bc")
        for v, spread in enumerate((lnw_bc, lnb_bc)):
            nc.tensor.matmul(out=spread[:], lhsT=ones_sq[:], rhs=vec_rows[:, v, :], start=True, stop=True)

        bn_s = keep.tile([P, PAIRS, 2, 2, 3], F32, name="bn_s")
        bn_e = keep.tile([P, TILES, 3], F32, name="bn_e")
        squares = keep.tile([P, TILES, ED - E1], F32, name="squares")
        square_sum = keep.tile([P, 2, TILES], F32, name="square_sum")
        norms = keep.tile([P, TILES, M1 + M2], F32, name="norms")
        part1 = keep.tile([P, TILES, M1], F32, name="part1")
        part2 = keep.tile([P, TILES, M2, 2], F32, name="part2")

        def component_sums(engine, first, last):
            two = slice(first, last)
            sq1 = squares[:, two, 0 : E2 - E1].rearrange("p i (c d) -> p i c d", d=D1)
            sq2 = squares[:, two, E2 - E1 :].rearrange("p i (c d) -> p i c d", d=D2)
            engine.tensor_tensor(out=part1[:, two, :], in0=sq1[:, :, :, 0], in1=sq1[:, :, :, 1], op=ALU.add)
            engine.tensor_tensor(out=part2[:, two, :, :], in0=sq2[:, :, :, 0:2], in1=sq2[:, :, :, 2:4], op=ALU.add)
            engine.tensor_tensor(out=norms[:, two, 0:M1], in0=part1[:, two, :], in1=sq1[:, :, :, 2], op=ALU.add)
            engine.tensor_tensor(out=part2[:, two, :, 0], in0=part2[:, two, :, 0], in1=part2[:, two, :, 1], op=ALU.add)
            engine.tensor_tensor(out=norms[:, two, M1:], in0=part2[:, two, :, 0], in1=sq2[:, :, :, 4], op=ALU.add)

        mean_var = keep.tile([P, TILES, 2], F32, name="mean_var")
        half_tiles = TILES // 2
        for lo in (0, half_tiles):
            for i in range(lo, lo + half_tiles):
                if i % 2 == 0:
                    two = slice(i, i + 2)
                    for part, columns in enumerate((slice(0, BN_COLUMNS), slice(BN_COLUMNS, S))):
                        nc.vector.bn_stats(
                            out=bn_s[:, i // 2, part, :, :].rearrange("p i f -> p (i f)"),
                            in_=x_s[:, two, columns].rearrange("p i s -> p s i"),
                        )
                    nc.vector.bn_stats(
                        out=bn_e[:, two, :].rearrange("p i f -> p (i f)"), in_=x_e[:, two, 0:M0].rearrange("p i s -> p s i")
                    )
                nc.scalar.activation(
                    out=squares[:, i, 0 : E2 - E1], in_=x_e[:, i, E1:E2], func=ACT.Square,
                    scale=D1**-0.25, accum_out=square_sum[:, 0, i : i + 1],
                )
                nc.scalar.activation(
                    out=squares[:, i, E2 - E1 :], in_=x_e[:, i, E2:ED], func=ACT.Square,
                    scale=D2**-0.25, accum_out=square_sum[:, 1, i : i + 1],
                )
            component_sums(nc.gpsimd, lo, lo + half_tiles)
        for i in range(TILES):
            nc.vector.bn_aggr(out=mean_var[:, i, :], in_=bn_s[:, i // 2, :, i % 2, :])
        std = keep.tile([P, 4, TILES], F32, name="std")
        nc.scalar.activation(
            out=std[:, 2, :], in_=square_sum[:, 0, :], func=ACT.Sqrt, scale=math.sqrt(D1) / M1, bias=eps_col[:]
        )
        nc.scalar.activation(
            out=std[:, 3, :], in_=square_sum[:, 1, :], func=ACT.Sqrt, scale=math.sqrt(D2) / M2, bias=eps_col[:]
        )
        nc.scalar.activation(out=std[:, 1, :], in_=bn_e[:, :, 2], func=ACT.Sqrt, scale=1.0 / M0, bias=eps_col[:])
        nc.scalar.activation(out=std[:, 0, :], in_=mean_var[:, :, 1], func=ACT.Sqrt, bias=eps_col[:])
        nc.scalar.activation(out=warm[:], in_=one_col[:], func=ACT.Silu)
        rstd = keep.tile([P, 4, TILES], F32, name="rstd")
        shift0 = keep.tile([P, TILES], F32, name="shift0")
        rvar = keep.tile([P, 2, TILES], F32, name="rvar")

        def after_std():
            nc.vector.reciprocal(out=rstd[:], in_=std[:])
            nc.vector.scalar_tensor_tensor(
                out=shift0[:], in0=bn_e[:, :, 1], scalar=-1.0, in1=rstd[:, 1, :], op0=ALU.mult, op1=ALU.mult
            )
            nc.vector.tensor_tensor(out=rvar[:], in0=rstd[:, 2:4, :], in1=rstd[:, 2:4, :], op=ALU.mult)

        addend_of = {}

        def add_node_scalar(pair):
            if pair < PAIRS - 2:
                addend = keep.tile([P, 2, S], F32, name="addend%d" % pair, align_bytes=64)
            else:
                addend = keep.tile([P, 2, S], F32, name="late%d" % pair, align_bytes=64)
            engine = nc.vector if pair == 1 else nc.gpsimd
            engine.tensor_tensor(
                out=addend[:], in0=x_s[:, 2 * pair : 2 * pair + 2, :],
                in1=b2_bc[:, 0:S].unsqueeze(1).to_broadcast([P, 2, S]), op=ALU.add,
            )
            addend_of[pair] = addend

        add_node_scalar(0)

        w1_words, w1_plane = weights[0]
        w2_words, w2_plane = weights[1]
        w1p_words = keep.tile([P, C], U32, name="w1p_words", align_bytes=64)
        w1p_plane = keep.tile([P, C], U8, name="w1p_plane", align_bytes=64)

        def permute_w1():
            nc.vector.tensor_copy(
                out=w1p_words[:].bitcast(I32).rearrange("p (t m) -> p t m", t=4),
                in_=w1_words[:].bitcast(I32).rearrange("p (m t) -> p t m", t=4),
            )
            nc.vector.tensor_copy(
                out=w1p_plane[:].rearrange("p (t m) -> p m t", t=4),
                in_=w1_plane[:].rearrange("p (m t) -> p m t", t=4),
            )

        centred = keep.tile([P, TILES, S], F32, name="centred")
        cat = keep.tile([P, TILES, C], BF16, name="cat", align_bytes=64)
        codes = keep.tile([P, 2, PAIRS, 2 * P], U32, name="codes", align_bytes=64)
        planes = keep.tile([P, 2, PAIRS, 2 * P], U8, name="planes", align_bytes=64)
        res_s = keep.tile([P, TILES, S], F32, name="res_s")
        res_e = keep.tile([P, TILES, ED], F32, name="res_e")
        blocks = ((0, M0, 1), (M0, M0 + M1, 2), (M0 + M1, NI, 3))
        turned_of = {}
        grouped_of = {}
        acc_of = {}
        hid_of = {}
        h_of = {}
        hidden_of = {}

        def invariants(pair):
            for i in both(pair):
                nc.scalar.activation(
                    out=cat[:, i, S : S + M0], in_=x_e[:, i, 0:M0], func=ACT.Square,
                    scale=rstd[:, 1, i : i + 1], bias=shift0[:, i : i + 1],
                )
                nc.scalar.activation(
                    out=cat[:, i, S + M0 : S + M0 + M1], in_=norms[:, i, 0:M1], func=ACT.Copy,
                    scale=rvar[:, 0, i : i + 1],
                )
                nc.scalar.activation(
                    out=cat[:, i, S + M0 + M1 :], in_=norms[:, i, M1:], func=ACT.Copy,
                    scale=rvar[:, 1, i : i + 1],
                )

        def centre(pair):
            for i in both(pair):
                nc.vector.scalar_tensor_tensor(
                    out=centred[:, i, :], in0=x_s[:, i, :], scalar=mean_var[:, i, 0:1], in1=lnw_bc[:, 0:S],
                    op0=ALU.subtract, op1=ALU.mult,
                )

        def layer_norm(pair):
            for i in both(pair):
                nc.vector.scalar_tensor_tensor(
                    out=cat[:, i, 0:S], in0=centred[:, i, :], scalar=rstd[:, 0, i : i + 1], in1=lnb_bc[:, 0:S],
                    op0=ALU.mult, op1=ALU.add,
                )

        def turn(pair):
            turned = psum_t.tile([P, 2, 2 * P], F32, name="turned")
            for half, i in enumerate(both(pair)):
                words = cat[:, i, :].bitcast(F32)
                for u in range(2):
                    nc.tensor.transpose(turned[:, u, half * P : (half + 1) * P], words[:, u : C // 2 : 2], ident[:])
            turned_of[pair] = turned

        def keep_warm(i):
            spare = psum_mm.tile([P, C], F32, name="acc")
            nc.tensor.matmul(out=spare[:], lhsT=ones_sq[:], rhs=cat[:, i, :], start=True, stop=True)

        def copy_out_cat(pair):
            if pair < PAIRS - 2:
                grouped = work.tile([P, 2 * P, 4], BF16, name="grouped", align_bytes=64)
            else:
                grouped = keep.tile([P, 2 * P, 4], BF16, name="late%d" % pair, align_bytes=64)
            nc.scalar.copy(
                out=grouped[:].rearrange("p r t -> p (r t)").bitcast(F32).rearrange("p (r u) -> p r u", u=2),
                in_=turned_of[pair][:].rearrange("p u r -> p r u"),
            )
            grouped_of[(0, pair)] = grouped

        def quantise(layer, pair):
            nc.vector.quantize_mx(
                out=codes[:, layer, pair, :].bitcast(FP8X4),
                scales=planes[:, layer, pair, :],
                in_=grouped_of[(layer, pair)][:].rearrange("p r t -> p (r t)"),
            )

        def first_layer(pair):
            quantise(0, pair)
            for u in range(2):
                hid = psum_mm.tile([P, 2, 2 * P], F32, name="hid")
                for e in range(2):
                    t = 2 * u + e
                    nc.tensor.matmul_mx(
                        out=hid[:, e, :],
                        lhsT=w1p_words[:, t * P : (t + 1) * P].bitcast(FP8X4),
                        lhsT_scale=w1p_plane[:, t * P : (t + 1) * P],
                        rhs=codes[:, 0, pair, :].bitcast(FP8X4),
                        rhs_scale=planes[:, 0, pair, :],
                        start=True,
                        stop=True,
                    )
                hid_of[(pair, u)] = hid

        def activate(pair):
            hidden = work.tile([P, 4, 2 * P], BF16, name="hidden")
            for t in range(4):
                nc.scalar.activation(
                    out=hidden[:, t, :], in_=hid_of[(pair, t // 2)][:, t % 2, :], func=ACT.Silu,
                    bias=b1_col[:, t : t + 1],
                )
            hidden_of[pair] = hidden

        def interleave(pair):
            grouped = work.tile([P, 2 * P, 4], BF16, name="grouped", align_bytes=64)
            copy = nc.vector.tensor_copy if pair == 0 else nc.scalar.copy
            copy(out=grouped[:], in_=hidden_of[pair][:].rearrange("p t r -> p r t"))
            grouped_of[(1, pair)] = grouped

        def second_layer(pair):
            quantise(1, pair)
            for half, i in enumerate(both(pair)):
                acc = psum_mm.tile([P, C], F32, name="acc")
                nc.tensor.matmul_mx(
                    out=acc[:],
                    lhsT=codes[:, 1, pair, half * P : (half + 1) * P].bitcast(FP8X4),
                    lhsT_scale=planes[:, 1, pair, half * P : (half + 1) * P],
                    rhs=w2_words[:].bitcast(FP8X4),
                    rhs_scale=w2_plane[:],
                    start=True,
                    stop=True,
                )
                acc_of[i] = acc

        def add_up(pair):
            for i in both(pair):
                h = keep.tile([P, NI], F32, name="h%d" % i)
                nc.vector.tensor_tensor(out=res_s[:, i, :], in0=acc_of[i][:, 0:S], in1=addend_of[pair][:, i % 2, :], op=ALU.add)
                for lo, hi, kind in blocks:
                    nc.vector.scalar_tensor_tensor(
                        out=h[:, lo:hi], in0=acc_of[i][:, S + lo : S + hi], scalar=std[:, kind, i : i + 1],
                        in1=b2_bc[:, S + lo : S + hi], op0=ALU.add, op1=ALU.add,
                    )
                h_of[i] = h
            two = slice(2 * pair, 2 * pair + 2)
            nc.sync.dma_start(out=out_dram[:, two, 0:S], in_=res_s[:, two, :])

        def gate(pair):
            for i in both(pair):
                nc.vector.scalar_tensor_tensor(
                    out=res_e[:, i, 0:M0], in0=x_e[:, i, 0:M0], scalar=bn_e[:, i, 1:2],
                    in1=h_of[i][:, 0:M0], op0=ALU.subtract, op1=ALU.mult,
                )
                nc.vector.scalar_tensor_tensor(
                    out=res_e[:, i, E1:E2].rearrange("p (c d) -> p c d", d=D1),
                    in0=h_of[i][:, M0 : M0 + M1].unsqueeze(2).to_broadcast([P, M1, D1]),
                    scalar=rstd[:, 2, i : i + 1],
                    in1=x_e[:, i, E1:E2].rearrange("p (c d) -> p c d", d=D1),
                    op0=ALU.mult, op1=ALU.mult,
                )
                nc.vector.scalar_tensor_tensor(
                    out=res_e[:, i, E2:].rearrange("p (c d) -> p c d", d=D2),
                    in0=h_of[i][:, M0 + M1 :].unsqueeze(2).to_broadcast([P, M2, D2]),
                    scalar=rstd[:, 3, i : i + 1],
                    in1=x_e[:, i, E2:ED].rearrange("p (c d) -> p c d", d=D2),
                    op0=ALU.mult, op1=ALU.mult,
                )

        def mean_back(pair):
            for i in both(pair):
                nc.scalar.activation(
                    out=res_e[:, i, 0:M0], in_=res_e[:, i, 0:M0], func=ACT.Identity,
                    scale=rstd[:, 1, i : i + 1], bias=bn_e[:, i, 1:2],
                )
                nc.sync.dma_start(out=out_dram[:, i, S:], in_=res_e[:, i, :])

        centre(0)
        after_std()
        invariants(0)
        layer_norm(0)
        turn(0)
        keep_warm(0)
        keep_warm(1)
        invariants(1)
        centre(1)
        layer_norm(1)
        turn(1)
        keep_warm(3)
        permute_w1()
        copy_out_cat(0)
        first_layer(0)
        centre(2)
        layer_norm(2)
        copy_out_cat(1)
        first_layer(1)
        centre(3)
        layer_norm(3)
        activate(0)
        invariants(2)
        turn(2)
        keep_warm(4)
        invariants(3)
        turn(3)
        for pair in range(PAIRS + 1):
            if pair < PAIRS:
                interleave(pair)
            if pair >= 1:
                add_up(pair - 1)
            if pair < PAIRS:
                second_layer(pair)
            if pair == 0:
                add_node_scalar(1)
            if pair + 2 < PAIRS:
                copy_out_cat(pair + 2)
            if pair >= 1:
                gate(pair - 1)
            if pair + 2 < PAIRS:
                first_layer(pair + 2)
                add_node_scalar(pair + 2)
            if pair + 1 < PAIRS:
                activate(pair + 1)
            if pair >= 1:
                mean_back(pair - 1)
